import numpy as np
import ml_dtypes


def mxq(x, axis, fmt="e4m3"):
    dtype, down = {"e4m3": (ml_dtypes.float8_e4m3fn, 7), "e5m2": (ml_dtypes.float8_e5m2, 14)}[fmt]
    v = np.moveaxis(np.asarray(x, np.float32).astype(ml_dtypes.bfloat16).astype(np.float64), axis, -1)
    blocks = v.reshape(v.shape[:-1] + (-1, 32))
    amax = np.abs(blocks).max(-1, keepdims=True)
    byte = np.maximum(np.where(amax > 0, np.frexp(amax)[1] - 1 + 127, 0) - down, 1)
    scale = np.exp2(byte - 127.0)
    codes = (blocks / scale).astype(np.float32).astype(dtype).astype(np.float64)
    return np.moveaxis((codes * scale).reshape(v.shape), -1, axis)


WIDE = False


def mx_kscale(k):
    if not WIDE:
        return np.ones(k)
    levels = np.array([10, -10, 5, -5, 0])
    a = np.random.permutation(np.resize(levels, k // 512 * 4)).reshape(k // 512, 4)
    idx = np.arange(k)
    return np.exp2(a[idx // 512, idx % 128 // 32])


BF16 = ml_dtypes.bfloat16


def bf(x):
    return np.asarray(x, np.float32).astype(BF16)


def f64(x):
    return np.asarray(x).astype(np.float64)


B, R, C0, C1, C2, H0, H1, H2 = 20, 128, 512, 1024, 2048, 32, 16, 8
EPS = 1e-12
MU = 0.5
P = H0 // H1
N0, N1 = H0 * H0, H1 * H1


def setup_inputs():
    s0, s1 = mx_kscale(C0), mx_kscale(C1)
    return {"fmap_low": bf((np.random.standard_normal((B, C0, H0, H0)) + MU) * s0[None, :, None, None]),
            "w_low": bf(np.random.standard_normal((R, C0)) / np.sqrt(C0) / s0[None, :]),
            "fmap_high": bf((np.random.standard_normal((B, C1, H1, H1)) + MU) * s1[None, :, None, None]),
            "w_high": bf(np.random.standard_normal((R, C1)) / np.sqrt(C1) / s1[None, :])}


def cam(fmap, w, c, n):
    return mxq(f64(w), 1, "e4m3") @ mxq(f64(fmap).reshape(B, c, n), 1, "e4m3")


def unit(v):
    return v / np.maximum(np.sqrt((v * v).sum(-1, keepdims=True)), EPS)


def reference(fmap_low, w_low, fmap_high, w_high):
    low = cam(fmap_low, w_low, C0, N0)
    high = cam(fmap_high, w_high, C1, N1)
    low = low.reshape(B, R, H1, P, H1, P).mean(axis=(3, 5)).reshape(B, R, N1)
    lo = unit(low).transpose(1, 0, 2).reshape(R, B * N1)
    hi = unit(high).transpose(1, 0, 2).reshape(R, B * N1)
    return (mxq(lo, 1, "e4m3") @ mxq(hi, 1, "e4m3").T) / B

@@ -1,0 +1,247 @@
+from contextlib import ExitStack
+
+import concourse.masks as masks
+import concourse.mybir as mybir
+
+F32 = mybir.dt.float32
+BF16 = mybir.dt.bfloat16
+U32 = mybir.dt.uint32
+U8 = mybir.dt.uint8
+FP8X4 = mybir.dt.float8_e4m3fn_x4
+ACT = mybir.ActivationFunctionType
+ALU = mybir.AluOpType
+
+P = 128
+PACK = 4
+K_PASS = P * PACK
+BATCH = 20
+C_LOW = 512
+C_HIGH = 1024
+SIDE = 16
+WIN = 2
+N_POS = SIDE * SIDE
+N_WIN = WIN * WIN
+N_LOW = N_POS * N_WIN
+HIGH_PASSES = C_HIGH // K_PASS
+W_PASSES = C_LOW // K_PASS + HIGH_PASSES
+LEVELS = 2
+PAIR = K_PASS // N_POS
+PAIRS = BATCH // PAIR
+P_SAMPLE = P // PAIR
+RUN = 4
+EPS = 1e-12
+
+FLOPS = 2 * P * BATCH * (C_LOW * N_LOW + C_HIGH * N_POS) + 2 * P * P * BATCH * N_POS
+
+
+def tile_avsl_graph_pa_kernel(tc, fmap_low, w_low, fmap_high, w_high, out):
+    nc = tc.nc
+    with ExitStack() as ctx:
+        ctx.enter_context(tc.manual_schedule())
+        consts = ctx.enter_context(tc.tile_pool(name="consts", bufs=1))
+        raw = ctx.enter_context(tc.tile_pool(name="raw", bufs=4))
+        grouped = ctx.enter_context(tc.tile_pool(name="grouped", bufs=2))
+        quantised = ctx.enter_context(tc.tile_pool(name="quantised", bufs=2))
+        scratch = ctx.enter_context(tc.tile_pool(name="scratch", bufs=4))
+        small = ctx.enter_context(tc.tile_pool(name="small", bufs=2))
+        psum_cam = ctx.enter_context(tc.psum_pool(name="psum_cam", bufs=4))
+        psum_turn = ctx.enter_context(tc.psum_pool(name="psum_turn", bufs=2))
+        psum_link = ctx.enter_context(tc.psum_pool(name="psum_link", bufs=1))
+
+        identity = consts.tile([P, P], BF16, name="identity")
+        masks.make_identity(nc, identity[:])
+        floor = consts.tile([P, PAIR, LEVELS], F32, name="floor")
+        nc.vector.memset(floor[:, :, 0:1], (N_WIN * EPS) ** 2)
+        nc.vector.memset(floor[:, :, 1:2], EPS**2)
+
+        w_rows = consts.tile([P, W_PASSES * K_PASS], BF16, name="w_rows")
+        nc.sync.dma_start(out=w_rows[:, 0:C_LOW], in_=w_low)
+        nc.sync.dma_start(out=w_rows[:, C_LOW:], in_=w_high)
+        w_sorted = consts.tile([P, W_PASSES, PACK, P], BF16, name="w_sorted")
+        nc.vector.tensor_copy(
+            out=w_sorted[:], in_=w_rows[:].rearrange("r (g p t) -> r g t p", g=W_PASSES, t=PACK)
+        )
+        w_grouped = consts.tile([P, W_PASSES, P, PACK], BF16, name="w_grouped", align_bytes=64)
+        w_codes = consts.tile([P, W_PASSES, P], U32, name="w_codes", align_bytes=64)
+        w_scales = consts.tile([P, W_PASSES, P], U8, name="w_scales", align_bytes=64)
+        for g in range(W_PASSES):
+            w_turned = psum_turn.tile([P, PACK, P], BF16, name="w_turned", tag="turned")
+            for t in range(PACK):
+                nc.tensor.transpose(w_turned[:, t, :], w_sorted[:, g, t, :], identity[:])
+            nc.scalar.copy(out=w_grouped[:, g], in_=w_turned[:].rearrange("p t r -> p r t"))
+            nc.vector.quantize_mx(
+                out=w_codes[:, g, :].bitcast(FP8X4),
+                scales=w_scales[:, g, :],
+                in_=w_grouped[:, g].rearrange("p r t -> p (r t)"),
+            )
+
+        low_raw, high_raw, low_grouped, high_grouped = {}, {}, {}, {}
+        low_codes, low_scales, high_codes, high_scales = {}, {}, {}, {}
+        cam, sumsq, inverse, unit_sorted, unit_turned, unit_grouped = {}, {}, {}, {}, {}, {}
+        link = psum_link.tile([P, P], F32, name="link")
+
+        def load(b):
+            low_raw[b] = raw.tile([P, PACK, N_LOW], BF16, name="low_raw")
+            nc.sync.dma_start(out=low_raw[b][:], in_=fmap_low[b].rearrange("(p t) y x -> p t (y x)", t=PACK))
+            high_raw[b] = raw.tile([P, HIGH_PASSES, PACK, N_POS], BF16, name="high_raw")
+            nc.sync.dma_start(
+                out=high_raw[b][:],
+                in_=fmap_high[b].rearrange("(g p t) y x -> p g t (y x)", g=HIGH_PASSES, t=PACK),
+            )
+
+        def regroup_high(b):
+            high_grouped[b] = grouped.tile(
+                [P, HIGH_PASSES, N_POS, PACK], BF16, name="high_grouped", align_bytes=64
+            )
+            for g in range(HIGH_PASSES):
+                nc.scalar.copy(
+                    out=high_grouped[b][:, g].rearrange("p (c i) t -> p c t i", i=RUN),
+                    in_=high_raw[b][:, g].rearrange("p t (c i) -> p c t i", i=RUN),
+                )
+
+        def regroup_low(b):
+            low_grouped[b] = grouped.tile([P, N_WIN, N_POS, PACK], BF16, name="low_grouped", align_bytes=64)
+            source = low_raw[b][:].rearrange(
+                "p t (yy dy xx dx) -> p dy yy xx t dx", dy=WIN, xx=SIDE, dx=WIN
+            )
+            target = low_grouped[b][:].rearrange(
+                "p (dy dx) (yy xx) t -> p dy yy xx t dx", dy=WIN, xx=SIDE
+            )
+            for dy in range(WIN):
+                nc.vector.tensor_copy(out=target[:, dy], in_=source[:, dy])
+
+        def quantise(b):
+            high_codes[b] = quantised.tile([P, HIGH_PASSES * N_POS], U32, name="high_codes", align_bytes=64)
+            high_scales[b] = quantised.tile([P, HIGH_PASSES * N_POS], U8, name="high_scales", align_bytes=64)
+            nc.vector.quantize_mx(
+                out=high_codes[b][:].bitcast(FP8X4),
+                scales=high_scales[b][:],
+                in_=high_grouped[b][:].rearrange("p g i t -> p (g i t)"),
+            )
+            low_codes[b] = quantised.tile([P, N_LOW], U32, name="low_codes", align_bytes=64)
+            low_scales[b] = quantised.tile([P, N_LOW], U8, name="low_scales", align_bytes=64)
+            nc.vector.quantize_mx(
+                out=low_codes[b][:].bitcast(FP8X4),
+                scales=low_scales[b][:],
+                in_=low_grouped[b][:].rearrange("p w i t -> p (w i t)"),
+            )
+
+        def multiply(b):
+            cam[b] = psum_cam.tile([P, LEVELS, N_POS], F32, name="cam")
+            for w in range(N_WIN):
+                cols = slice(w * N_POS, (w + 1) * N_POS)
+                nc.tensor.matmul_mx(
+                    out=cam[b][:, 0, :],
+                    lhsT=w_codes[:, 0, :].bitcast(FP8X4),
+                    lhsT_scale=w_scales[:, 0, :],
+                    rhs=low_codes[b][:, cols].bitcast(FP8X4),
+                    rhs_scale=low_scales[b][:, cols],
+                    start=(w == 0),
+                    stop=(w == N_WIN - 1),
+                )
+            for g in range(HIGH_PASSES):
+                cols = slice(g * N_POS, (g + 1) * N_POS)
+                nc.tensor.matmul_mx(
+                    out=cam[b][:, 1, :],
+                    lhsT=w_codes[:, 1 + g, :].bitcast(FP8X4),
+                    lhsT_scale=w_scales[:, 1 + g, :],
+                    rhs=high_codes[b][:, cols].bitcast(FP8X4),
+                    rhs_scale=high_scales[b][:, cols],
+                    start=(g == 0),
+                    stop=(g == HIGH_PASSES - 1),
+                )
+
+        def sum_squares(b):
+            j, e = divmod(b, PAIR)
+            if e == 0:
+                sumsq[j] = small.tile([P, PAIR, LEVELS], F32, name="sumsq")
+            for level in range(LEVELS):
+                squares = scratch.tile([P, N_POS], BF16, name="squares")
+                nc.scalar.activation(
+                    out=squares[:],
+                    in_=cam[b][:, level, :],
+                    func=ACT.Square,
+                    accum_out=sumsq[j][:, e, level : level + 1],
+                )
+
+        def inverse_squares(j):
+            clamped = small.tile([P, PAIR, LEVELS], F32, name="clamped")
+            nc.vector.tensor_tensor(out=clamped[:], in0=sumsq[j][:], in1=floor[:], op=ALU.max)
+            inverse[j] = small.tile([P, PAIR, LEVELS], F32, name="inverse")
+            nc.vector.reciprocal(out=inverse[j][:], in_=clamped[:])
+
+        def normalise(j):
+            inverse_norm = small.tile([P, PAIR, LEVELS], F32, name="inverse_norm")
+            nc.scalar.activation(out=inverse_norm[:], in_=inverse[j][:], func=ACT.Sqrt)
+            unit_sorted[j] = grouped.tile([P, LEVELS, PACK, P], BF16, name="unit_sorted")
+            for e in range(PAIR):
+                for level in range(LEVELS):
+                    nc.scalar.activation(
+                        out=unit_sorted[j][:, level, :, e * P_SAMPLE : (e + 1) * P_SAMPLE],
+                        in_=cam[PAIR * j + e][:, level, :].rearrange("r (p t) -> r t p", t=PACK),
+                        func=ACT.Copy,
+                        scale=inverse_norm[:, e, level : level + 1],
+                    )
+
+        def turn(j):
+            unit_turned[j] = psum_turn.tile([P, LEVELS, PACK, P], BF16, name="unit_turned", tag="turned")
+            for level in range(LEVELS):
+                for t in range(PACK):
+                    nc.tensor.transpose(unit_turned[j][:, level, t, :], unit_sorted[j][:, level, t, :], identity[:])
+
+        def regroup_unit(j):
+            unit_grouped[j] = grouped.tile([P, LEVELS, P, PACK], BF16, name="unit_grouped", align_bytes=64)
+            nc.scalar.copy(out=unit_grouped[j][:], in_=unit_turned[j][:].rearrange("p l t r -> p l r t"))
+
+        def link_pass(j):
+            unit_codes = quantised.tile([P, LEVELS * P], U32, name="unit_codes", align_bytes=64)
+            unit_scales = quantised.tile([P, LEVELS * P], U8, name="unit_scales", align_bytes=64)
+            nc.vector.quantize_mx(
+                out=unit_codes[:].bitcast(FP8X4),
+                scales=unit_scales[:],
+                in_=unit_grouped[j][:].rearrange("p l r t -> p (l r t)"),
+            )
+            nc.tensor.matmul_mx(
+                out=link[:],
+                lhsT=unit_codes[:, 0:P].bitcast(FP8X4),
+                lhsT_scale=unit_scales[:, 0:P],
+                rhs=unit_codes[:, P:].bitcast(FP8X4),
+                rhs_scale=unit_scales[:, P:],
+                start=(j == 0),
+                stop=(j == PAIRS - 1),
+            )
+
+        def pair_at(step, lag):
+            j, odd = divmod(step - lag, PAIR)
+            return j if odd == 0 and 0 <= j < PAIRS else None
+
+        load(0)
+        regroup_high(0)
+        for step in range(BATCH + 4):
+            if step + 1 < BATCH:
+                load(step + 1)
+                regroup_high(step + 1)
+            if step < BATCH:
+                regroup_low(step)
+            j = pair_at(step, 5)
+            if j is not None:
+                link_pass(j)
+            if step < BATCH:
+                quantise(step)
+                multiply(step)
+            if 1 <= step <= BATCH:
+                sum_squares(step - 1)
+            j = pair_at(step, 2)
+            if j is not None:
+                inverse_squares(j)
+            j = pair_at(step, 3)
+            if j is not None:
+                normalise(j)
+                turn(j)
+            j = pair_at(step, 4)
+            if j is not None:
+                regroup_unit(j)
+
+        result = consts.tile([P, P], F32, name="result")
+        nc.scalar.activation(out=result[:], in_=link[:], func=ACT.Copy, scale=1.0 / BATCH)
+        nc.sync.dma_start(out=out, in_=result[:])

@@ -37,15 +37,14 @@ FLOPS = 2 * P * BATCH * (C_LOW * N_LOW + C_HIGH * N_POS) + 2 * P * P * BATCH * N
 def tile_avsl_graph_pa_kernel(tc, fmap_low, w_low, fmap_high, w_high, out):
     nc = tc.nc
     with ExitStack() as ctx:
-        ctx.enter_context(tc.manual_schedule())
         consts = ctx.enter_context(tc.tile_pool(name="consts", bufs=1))
-        raw = ctx.enter_context(tc.tile_pool(name="raw", bufs=4))
-        grouped = ctx.enter_context(tc.tile_pool(name="grouped", bufs=2))
-        quantised = ctx.enter_context(tc.tile_pool(name="quantised", bufs=2))
+        raw = ctx.enter_context(tc.tile_pool(name="raw", bufs=6))
+        grouped = ctx.enter_context(tc.tile_pool(name="grouped", bufs=3))
+        quantised = ctx.enter_context(tc.tile_pool(name="quantised", bufs=3))
         scratch = ctx.enter_context(tc.tile_pool(name="scratch", bufs=4))
-        small = ctx.enter_context(tc.tile_pool(name="small", bufs=2))
-        psum_cam = ctx.enter_context(tc.psum_pool(name="psum_cam", bufs=4))
-        psum_turn = ctx.enter_context(tc.psum_pool(name="psum_turn", bufs=2))
+        small = ctx.enter_context(tc.tile_pool(name="small", bufs=3))
+        psum_cam = ctx.enter_context(tc.psum_pool(name="psum_cam", bufs=3))
+        psum_turn = ctx.enter_context(tc.psum_pool(name="psum_turn", bufs=4))
         psum_link = ctx.enter_context(tc.psum_pool(name="psum_link", bufs=1))
 
         identity = consts.tile([P, P], BF16, name="identity")
@@ -55,25 +54,29 @@ def tile_avsl_graph_pa_kernel(tc, fmap_low, w_low, fmap_high, w_high, out):
         nc.vector.memset(floor[:, :, 1:2], EPS**2)
 
         w_rows = consts.tile([P, W_PASSES * K_PASS], BF16, name="w_rows")
-        nc.sync.dma_start(out=w_rows[:, 0:C_LOW], in_=w_low)
-        nc.sync.dma_start(out=w_rows[:, C_LOW:], in_=w_high)
-        w_sorted = consts.tile([P, W_PASSES, PACK, P], BF16, name="w_sorted")
-        nc.vector.tensor_copy(
-            out=w_sorted[:], in_=w_rows[:].rearrange("r (g p t) -> r g t p", g=W_PASSES, t=PACK)
-        )
         w_grouped = consts.tile([P, W_PASSES, P, PACK], BF16, name="w_grouped", align_bytes=64)
         w_codes = consts.tile([P, W_PASSES, P], U32, name="w_codes", align_bytes=64)
         w_scales = consts.tile([P, W_PASSES, P], U8, name="w_scales", align_bytes=64)
-        for g in range(W_PASSES):
-            w_turned = psum_turn.tile([P, PACK, P], BF16, name="w_turned", tag="turned")
-            for t in range(PACK):
-                nc.tensor.transpose(w_turned[:, t, :], w_sorted[:, g, t, :], identity[:])
-            nc.scalar.copy(out=w_grouped[:, g], in_=w_turned[:].rearrange("p t r -> p r t"))
-            nc.vector.quantize_mx(
-                out=w_codes[:, g, :].bitcast(FP8X4),
-                scales=w_scales[:, g, :],
-                in_=w_grouped[:, g].rearrange("p r t -> p (r t)"),
-            )
+
+        def load_weights():
+            nc.sync.dma_start(out=w_rows[:, 0:C_LOW], in_=w_low)
+            nc.sync.dma_start(out=w_rows[:, C_LOW:], in_=w_high)
+
+        def turn_weights():
+            w_by_t = w_rows[:].rearrange("r (g p t) -> r g t p", g=W_PASSES, t=PACK)
+            for g in range(W_PASSES):
+                w_turned = psum_turn.tile([P, PACK, P], BF16, name="w_turned", tag="turned")
+                for t in range(PACK):
+                    nc.tensor.transpose(w_turned[:, t, :], w_by_t[:, g, t, :], identity[:])
+                nc.scalar.copy(out=w_grouped[:, g], in_=w_turned[:].rearrange("p t r -> p r t"))
+
+        def quantise_weights():
+            for g in range(W_PASSES):
+                nc.vector.quantize_mx(
+                    out=w_codes[:, g, :].bitcast(FP8X4),
+                    scales=w_scales[:, g, :],
+                    in_=w_grouped[:, g].rearrange("p r t -> p (r t)"),
+                )
 
         low_raw, high_raw, low_grouped, high_grouped = {}, {}, {}, {}
         low_codes, low_scales, high_codes, high_scales = {}, {}, {}, {}
@@ -128,17 +131,6 @@ def tile_avsl_graph_pa_kernel(tc, fmap_low, w_low, fmap_high, w_high, out):
 
         def multiply(b):
             cam[b] = psum_cam.tile([P, LEVELS, N_POS], F32, name="cam")
-            for w in range(N_WIN):
-                cols = slice(w * N_POS, (w + 1) * N_POS)
-                nc.tensor.matmul_mx(
-                    out=cam[b][:, 0, :],
-                    lhsT=w_codes[:, 0, :].bitcast(FP8X4),
-                    lhsT_scale=w_scales[:, 0, :],
-                    rhs=low_codes[b][:, cols].bitcast(FP8X4),
-                    rhs_scale=low_scales[b][:, cols],
-                    start=(w == 0),
-                    stop=(w == N_WIN - 1),
-                )
             for g in range(HIGH_PASSES):
                 cols = slice(g * N_POS, (g + 1) * N_POS)
                 nc.tensor.matmul_mx(
@@ -149,6 +141,17 @@ def tile_avsl_graph_pa_kernel(tc, fmap_low, w_low, fmap_high, w_high, out):
                     rhs_scale=high_scales[b][:, cols],
                     start=(g == 0),
                     stop=(g == HIGH_PASSES - 1),
+                )
+            for w in range(N_WIN):
+                cols = slice(w * N_POS, (w + 1) * N_POS)
+                nc.tensor.matmul_mx(
+                    out=cam[b][:, 0, :],
+                    lhsT=w_codes[:, 0, :].bitcast(FP8X4),
+                    lhsT_scale=w_scales[:, 0, :],
+                    rhs=low_codes[b][:, cols].bitcast(FP8X4),
+                    rhs_scale=low_scales[b][:, cols],
+                    start=(w == 0),
+                    stop=(w == N_WIN - 1),
                 )
 
         def sum_squares(b):
@@ -170,28 +173,28 @@ def tile_avsl_graph_pa_kernel(tc, fmap_low, w_low, fmap_high, w_high, out):
             inverse[j] = small.tile([P, PAIR, LEVELS], F32, name="inverse")
             nc.vector.reciprocal(out=inverse[j][:], in_=clamped[:])
 
-        def normalise(j):
+        def normalise_and_turn(j):
             inverse_norm = small.tile([P, PAIR, LEVELS], F32, name="inverse_norm")
             nc.scalar.activation(out=inverse_norm[:], in_=inverse[j][:], func=ACT.Sqrt)
-            unit_sorted[j] = grouped.tile([P, LEVELS, PACK, P], BF16, name="unit_sorted")
-            for e in range(PAIR):
-                for level in range(LEVELS):
+            for level in range(LEVELS):
+                unit_sorted[j, level] = grouped.tile([P, PACK, P], BF16, name="unit_sorted")
+                for e in range(PAIR):
                     nc.scalar.activation(
-                        out=unit_sorted[j][:, level, :, e * P_SAMPLE : (e + 1) * P_SAMPLE],
+                        out=unit_sorted[j, level][:, :, e * P_SAMPLE : (e + 1) * P_SAMPLE],
                         in_=cam[PAIR * j + e][:, level, :].rearrange("r (p t) -> r t p", t=PACK),
                         func=ACT.Copy,
                         scale=inverse_norm[:, e, level : level + 1],
                     )
-
-        def turn(j):
-            unit_turned[j] = psum_turn.tile([P, LEVELS, PACK, P], BF16, name="unit_turned", tag="turned")
-            for level in range(LEVELS):
+                unit_turned[j, level] = psum_turn.tile([P, PACK, P], BF16, name="unit_turned", tag="turned")
                 for t in range(PACK):
-                    nc.tensor.transpose(unit_turned[j][:, level, t, :], unit_sorted[j][:, level, t, :], identity[:])
+                    nc.tensor.transpose(unit_turned[j, level][:, t, :], unit_sorted[j, level][:, t, :], identity[:])
 
         def regroup_unit(j):
             unit_grouped[j] = grouped.tile([P, LEVELS, P, PACK], BF16, name="unit_grouped", align_bytes=64)
-            nc.scalar.copy(out=unit_grouped[j][:], in_=unit_turned[j][:].rearrange("p l t r -> p l r t"))
+            for level in range(LEVELS):
+                nc.scalar.copy(
+                    out=unit_grouped[j][:, level], in_=unit_turned[j, level][:].rearrange("p t r -> p r t")
+                )
 
         def link_pass(j):
             unit_codes = quantised.tile([P, LEVELS * P], U32, name="unit_codes", align_bytes=64)
@@ -216,29 +219,33 @@ def tile_avsl_graph_pa_kernel(tc, fmap_low, w_low, fmap_high, w_high, out):
             return j if odd == 0 and 0 <= j < PAIRS else None
 
         load(0)
+        load_weights()
         regroup_high(0)
-        for step in range(BATCH + 4):
+        regroup_low(0)
+        turn_weights()
+        for step in range(BATCH + 3):
             if step + 1 < BATCH:
                 load(step + 1)
                 regroup_high(step + 1)
-            if step < BATCH:
-                regroup_low(step)
-            j = pair_at(step, 5)
+            j = pair_at(step, 4)
             if j is not None:
                 link_pass(j)
             if step < BATCH:
                 quantise(step)
+            if step == 0:
+                quantise_weights()
+            if step < BATCH:
                 multiply(step)
             if 1 <= step <= BATCH:
                 sum_squares(step - 1)
             j = pair_at(step, 2)
             if j is not None:
                 inverse_squares(j)
-            j = pair_at(step, 3)
+            if step + 1 < BATCH:
+                regroup_low(step + 1)
             if j is not None:
-                normalise(j)
-                turn(j)
-            j = pair_at(step, 4)
+                normalise_and_turn(j)
+            j = pair_at(step, 3)
             if j is not None:
                 regroup_unit(j)
 

@@ -37,6 +37,7 @@ FLOPS = 2 * P * BATCH * (C_LOW * N_LOW + C_HIGH * N_POS) + 2 * P * P * BATCH * N
 def tile_avsl_graph_pa_kernel(tc, fmap_low, w_low, fmap_high, w_high, out):
     nc = tc.nc
     with ExitStack() as ctx:
+        ctx.enter_context(tc.manual_schedule())
         consts = ctx.enter_context(tc.tile_pool(name="consts", bufs=1))
         raw = ctx.enter_context(tc.tile_pool(name="raw", bufs=6))
         grouped = ctx.enter_context(tc.tile_pool(name="grouped", bufs=3))
@@ -80,17 +81,17 @@ def tile_avsl_graph_pa_kernel(tc, fmap_low, w_low, fmap_high, w_high, out):
 
         low_raw, high_raw, low_grouped, high_grouped = {}, {}, {}, {}
         low_codes, low_scales, high_codes, high_scales = {}, {}, {}, {}
-        cam, sumsq, inverse, unit_sorted, unit_turned, unit_grouped = {}, {}, {}, {}, {}, {}
+        cam, sumsq, clamped, inverse, unit_sorted, unit_turned, unit_grouped = {}, {}, {}, {}, {}, {}, {}
         link = psum_link.tile([P, P], F32, name="link")
 
         def load(b):
-            low_raw[b] = raw.tile([P, PACK, N_LOW], BF16, name="low_raw")
-            nc.sync.dma_start(out=low_raw[b][:], in_=fmap_low[b].rearrange("(p t) y x -> p t (y x)", t=PACK))
             high_raw[b] = raw.tile([P, HIGH_PASSES, PACK, N_POS], BF16, name="high_raw")
             nc.sync.dma_start(
                 out=high_raw[b][:],
                 in_=fmap_high[b].rearrange("(g p t) y x -> p g t (y x)", g=HIGH_PASSES, t=PACK),
             )
+            low_raw[b] = raw.tile([P, PACK, N_LOW], BF16, name="low_raw")
+            nc.sync.dma_start(out=low_raw[b][:], in_=fmap_low[b].rearrange("(p t) y x -> p t (y x)", t=PACK))
 
         def regroup_high(b):
             high_grouped[b] = grouped.tile(
@@ -167,24 +168,28 @@ def tile_avsl_graph_pa_kernel(tc, fmap_low, w_low, fmap_high, w_high, out):
                     accum_out=sumsq[j][:, e, level : level + 1],
                 )
 
-        def inverse_squares(j):
-            clamped = small.tile([P, PAIR, LEVELS], F32, name="clamped")
-            nc.vector.tensor_tensor(out=clamped[:], in0=sumsq[j][:], in1=floor[:], op=ALU.max)
+        def clamp_squares(j):
+            clamped[j] = small.tile([P, PAIR, LEVELS], F32, name="clamped")
+            nc.vector.tensor_tensor(out=clamped[j][:], in0=sumsq[j][:], in1=floor[:], op=ALU.max)
+
+        def invert_squares(j):
             inverse[j] = small.tile([P, PAIR, LEVELS], F32, name="inverse")
-            nc.vector.reciprocal(out=inverse[j][:], in_=clamped[:])
+            nc.vector.reciprocal(out=inverse[j][:], in_=clamped[j][:])
 
         def normalise_and_turn(j):
             inverse_norm = small.tile([P, PAIR, LEVELS], F32, name="inverse_norm")
             nc.scalar.activation(out=inverse_norm[:], in_=inverse[j][:], func=ACT.Sqrt)
             for level in range(LEVELS):
                 unit_sorted[j, level] = grouped.tile([P, PACK, P], BF16, name="unit_sorted")
-                for e in range(PAIR):
+            for e in range(PAIR):
+                for level in range(LEVELS):
                     nc.scalar.activation(
                         out=unit_sorted[j, level][:, :, e * P_SAMPLE : (e + 1) * P_SAMPLE],
                         in_=cam[PAIR * j + e][:, level, :].rearrange("r (p t) -> r t p", t=PACK),
                         func=ACT.Copy,
                         scale=inverse_norm[:, e, level : level + 1],
                     )
+            for level in range(LEVELS):
                 unit_turned[j, level] = psum_turn.tile([P, PACK, P], BF16, name="unit_turned", tag="turned")
                 for t in range(PACK):
                     nc.tensor.transpose(unit_turned[j, level][:, t, :], unit_sorted[j, level][:, t, :], identity[:])
@@ -224,30 +229,32 @@ def tile_avsl_graph_pa_kernel(tc, fmap_low, w_low, fmap_high, w_high, out):
         regroup_low(0)
         turn_weights()
         for step in range(BATCH + 3):
+            if 1 <= step <= BATCH:
+                sum_squares(step - 1)
             if step + 1 < BATCH:
                 load(step + 1)
                 regroup_high(step + 1)
-            j = pair_at(step, 4)
-            if j is not None:
-                link_pass(j)
             if step < BATCH:
                 quantise(step)
             if step == 0:
                 quantise_weights()
             if step < BATCH:
                 multiply(step)
-            if 1 <= step <= BATCH:
-                sum_squares(step - 1)
-            j = pair_at(step, 2)
-            if j is not None:
-                inverse_squares(j)
+            normed = pair_at(step, 2)
+            if normed is not None:
+                clamp_squares(normed)
+            linked = pair_at(step, 4)
+            if linked is not None:
+                link_pass(linked)
+            if normed is not None:
+                invert_squares(normed)
             if step + 1 < BATCH:
                 regroup_low(step + 1)
-            if j is not None:
-                normalise_and_turn(j)
-            j = pair_at(step, 3)
-            if j is not None:
-                regroup_unit(j)
+            if normed is not None:
+                normalise_and_turn(normed)
+            turned = pair_at(step, 3)
+            if turned is not None:
+                regroup_unit(turned)
 
         result = consts.tile([P, P], F32, name="result")
         nc.scalar.activation(out=result[:], in_=link[:], func=ACT.Copy, scale=1.0 / BATCH)

@@ -9,7 +9,6 @@ U32 = mybir.dt.uint32
 U8 = mybir.dt.uint8
 FP8X4 = mybir.dt.float8_e4m3fn_x4
 ACT = mybir.ActivationFunctionType
-ALU = mybir.AluOpType
 
 P = 128
 PACK = 4
@@ -30,6 +29,7 @@ PAIRS = BATCH // PAIR
 P_SAMPLE = P // PAIR
 RUN = 4
 EPS = 1e-12
+TO_MEAN = (1.0 / N_WIN, 1.0)
 
 FLOPS = 2 * P * BATCH * (C_LOW * N_LOW + C_HIGH * N_POS) + 2 * P * P * BATCH * N_POS
 
@@ -50,9 +50,9 @@ def tile_avsl_graph_pa_kernel(tc, fmap_low, w_low, fmap_high, w_high, out):
 
         identity = consts.tile([P, P], BF16, name="identity")
         masks.make_identity(nc, identity[:])
-        floor = consts.tile([P, PAIR, LEVELS], F32, name="floor")
-        nc.vector.memset(floor[:, :, 0:1], (N_WIN * EPS) ** 2)
-        nc.vector.memset(floor[:, :, 1:2], EPS**2)
+        ones = consts.tile([P, 1], F32, name="ones")
+        nc.vector.memset(ones[:], 1.0)
+        nc.scalar.activation(out=ones[:], in_=ones[:], func=ACT.Abs_reciprocal_sqrt)
 
         w_rows = consts.tile([P, W_PASSES * K_PASS], BF16, name="w_rows")
         w_grouped = consts.tile([P, W_PASSES, P, PACK], BF16, name="w_grouped", align_bytes=64)
@@ -81,7 +81,7 @@ def tile_avsl_graph_pa_kernel(tc, fmap_low, w_low, fmap_high, w_high, out):
 
         low_raw, high_raw, low_grouped, high_grouped = {}, {}, {}, {}
         low_codes, low_scales, high_codes, high_scales = {}, {}, {}, {}
-        cam, sumsq, clamped, inverse, unit_sorted, unit_turned, unit_grouped = {}, {}, {}, {}, {}, {}, {}
+        cam, sumsq, clamped, inverse_norm, unit_sorted, unit_turned, unit_grouped = {}, {}, {}, {}, {}, {}, {}
         link = psum_link.tile([P, P], F32, name="link")
 
         def load(b):
@@ -93,15 +93,15 @@ def tile_avsl_graph_pa_kernel(tc, fmap_low, w_low, fmap_high, w_high, out):
             low_raw[b] = raw.tile([P, PACK, N_LOW], BF16, name="low_raw")
             nc.sync.dma_start(out=low_raw[b][:], in_=fmap_low[b].rearrange("(p t) y x -> p t (y x)", t=PACK))
 
-        def regroup_high(b):
-            high_grouped[b] = grouped.tile(
-                [P, HIGH_PASSES, N_POS, PACK], BF16, name="high_grouped", align_bytes=64
-            )
-            for g in range(HIGH_PASSES):
-                nc.scalar.copy(
-                    out=high_grouped[b][:, g].rearrange("p (c i) t -> p c t i", i=RUN),
-                    in_=high_raw[b][:, g].rearrange("p t (c i) -> p c t i", i=RUN),
+        def regroup_high(b, g):
+            if g == 0:
+                high_grouped[b] = grouped.tile(
+                    [P, HIGH_PASSES, N_POS, PACK], BF16, name="high_grouped", align_bytes=64
                 )
+            nc.scalar.copy(
+                out=high_grouped[b][:, g].rearrange("p (c i) t -> p c t i", i=RUN),
+                in_=high_raw[b][:, g].rearrange("p t (c i) -> p c t i", i=RUN),
+            )
 
         def regroup_low(b):
             low_grouped[b] = grouped.tile([P, N_WIN, N_POS, PACK], BF16, name="low_grouped", align_bytes=64)
@@ -165,20 +165,21 @@ def tile_avsl_graph_pa_kernel(tc, fmap_low, w_low, fmap_high, w_high, out):
                     out=squares[:],
                     in_=cam[b][:, level, :],
                     func=ACT.Square,
+                    scale=TO_MEAN[level],
                     accum_out=sumsq[j][:, e, level : level + 1],
                 )
 
         def clamp_squares(j):
             clamped[j] = small.tile([P, PAIR, LEVELS], F32, name="clamped")
-            nc.vector.tensor_tensor(out=clamped[j][:], in0=sumsq[j][:], in1=floor[:], op=ALU.max)
+            nc.scalar.activation(out=clamped[j][:], in_=sumsq[j][:], func=ACT.Relu, bias=-(EPS**2))
 
-        def invert_squares(j):
-            inverse[j] = small.tile([P, PAIR, LEVELS], F32, name="inverse")
-            nc.vector.reciprocal(out=inverse[j][:], in_=clamped[j][:])
+        def invert_norms(j):
+            inverse_norm[j] = small.tile([P, PAIR, LEVELS], F32, name="inverse_norm")
+            nc.scalar.activation(
+                out=inverse_norm[j][:], in_=clamped[j][:], func=ACT.Abs_reciprocal_sqrt, bias=EPS**2
+            )
 
         def normalise_and_turn(j):
-            inverse_norm = small.tile([P, PAIR, LEVELS], F32, name="inverse_norm")
-            nc.scalar.activation(out=inverse_norm[:], in_=inverse[j][:], func=ACT.Sqrt)
             for level in range(LEVELS):
                 unit_sorted[j, level] = grouped.tile([P, PACK, P], BF16, name="unit_sorted")
             for e in range(PAIR):
@@ -187,7 +188,7 @@ def tile_avsl_graph_pa_kernel(tc, fmap_low, w_low, fmap_high, w_high, out):
                         out=unit_sorted[j, level][:, :, e * P_SAMPLE : (e + 1) * P_SAMPLE],
                         in_=cam[PAIR * j + e][:, level, :].rearrange("r (p t) -> r t p", t=PACK),
                         func=ACT.Copy,
-                        scale=inverse_norm[:, e, level : level + 1],
+                        scale=inverse_norm[j][:, e, level : level + 1],
                     )
             for level in range(LEVELS):
                 unit_turned[j, level] = psum_turn.tile([P, PACK, P], BF16, name="unit_turned", tag="turned")
@@ -197,8 +198,11 @@ def tile_avsl_graph_pa_kernel(tc, fmap_low, w_low, fmap_high, w_high, out):
         def regroup_unit(j):
             unit_grouped[j] = grouped.tile([P, LEVELS, P, PACK], BF16, name="unit_grouped", align_bytes=64)
             for level in range(LEVELS):
-                nc.scalar.copy(
-                    out=unit_grouped[j][:, level], in_=unit_turned[j, level][:].rearrange("p t r -> p r t")
+                nc.scalar.activation(
+                    out=unit_grouped[j][:, level],
+                    in_=unit_turned[j, level][:].rearrange("p t r -> p r t"),
+                    func=ACT.Copy,
+                    scale=TO_MEAN[level],
                 )
 
         def link_pass(j):
@@ -225,34 +229,37 @@ def tile_avsl_graph_pa_kernel(tc, fmap_low, w_low, fmap_high, w_high, out):
 
         load(0)
         load_weights()
-        regroup_high(0)
+        regroup_high(0, 0)
+        regroup_high(0, 1)
         regroup_low(0)
         turn_weights()
         for step in range(BATCH + 3):
+            normed = pair_at(step, 2)
+            linked = pair_at(step, 4)
+            turned = pair_at(step, 3)
             if 1 <= step <= BATCH:
                 sum_squares(step - 1)
             if step + 1 < BATCH:
                 load(step + 1)
-                regroup_high(step + 1)
+                regroup_high(step + 1, 0)
+            if normed is not None:
+                clamp_squares(normed)
+            if step + 1 < BATCH:
+                regroup_high(step + 1, 1)
+            if normed is not None:
+                invert_norms(normed)
             if step < BATCH:
                 quantise(step)
             if step == 0:
                 quantise_weights()
             if step < BATCH:
                 multiply(step)
-            normed = pair_at(step, 2)
-            if normed is not None:
-                clamp_squares(normed)
-            linked = pair_at(step, 4)
             if linked is not None:
                 link_pass(linked)
-            if normed is not None:
-                invert_squares(normed)
             if step + 1 < BATCH:
                 regroup_low(step + 1)
             if normed is not None:
                 normalise_and_turn(normed)
-            turned = pair_at(step, 3)
             if turned is not None:
                 regroup_unit(turned)
 

@@ -21,12 +21,14 @@ WIN = 2
 N_POS = SIDE * SIDE
 N_WIN = WIN * WIN
 N_LOW = N_POS * N_WIN
+ROW_PAIR = N_LOW // SIDE
 HIGH_PASSES = C_HIGH // K_PASS
 W_PASSES = C_LOW // K_PASS + HIGH_PASSES
 LEVELS = 2
+BOTH = (0, 1)
+WORDS = 2
 PAIR = K_PASS // N_POS
 PAIRS = BATCH // PAIR
-P_SAMPLE = P // PAIR
 RUN = 4
 EPS = 1e-12
 TO_MEAN = (1.0 / N_WIN, 1.0)
@@ -50,6 +52,8 @@ def tile_avsl_graph_pa_kernel(tc, fmap_low, w_low, fmap_high, w_high, out):
 
         identity = consts.tile([P, P], BF16, name="identity")
         masks.make_identity(nc, identity[:])
+        identity_words = consts.tile([P, P], F32, name="identity_words")
+        masks.make_identity(nc, identity_words[:])
         ones = consts.tile([P, 1], F32, name="ones")
         nc.vector.memset(ones[:], 1.0)
         nc.scalar.activation(out=ones[:], in_=ones[:], func=ACT.Abs_reciprocal_sqrt)
@@ -81,17 +85,24 @@ def tile_avsl_graph_pa_kernel(tc, fmap_low, w_low, fmap_high, w_high, out):
 
         low_raw, high_raw, low_grouped, high_grouped = {}, {}, {}, {}
         low_codes, low_scales, high_codes, high_scales = {}, {}, {}, {}
-        cam, sumsq, clamped, inverse_norm, unit_sorted, unit_turned, unit_grouped = {}, {}, {}, {}, {}, {}, {}
+        cam, sumsq, clamped, inverse_norm, unit, unit_turned, unit_grouped = {}, {}, {}, {}, {}, {}, {}
+        unit_codes, unit_scales = {}, {}
         link = psum_link.tile([P, P], F32, name="link")
 
-        def load(b):
-            high_raw[b] = raw.tile([P, HIGH_PASSES, PACK, N_POS], BF16, name="high_raw")
+        def load_high(b, first=0, count=HIGH_PASSES):
+            if first == 0:
+                high_raw[b] = raw.tile([P, HIGH_PASSES, PACK, N_POS], BF16, name="high_raw")
+            channels = fmap_high[b].rearrange("(g p t) y x -> p g t (y x)", g=HIGH_PASSES, t=PACK)
             nc.sync.dma_start(
-                out=high_raw[b][:],
-                in_=fmap_high[b].rearrange("(g p t) y x -> p g t (y x)", g=HIGH_PASSES, t=PACK),
+                out=high_raw[b][:, first : first + count], in_=channels[:, first : first + count]
             )
-            low_raw[b] = raw.tile([P, PACK, N_LOW], BF16, name="low_raw")
-            nc.sync.dma_start(out=low_raw[b][:], in_=fmap_low[b].rearrange("(p t) y x -> p t (y x)", t=PACK))
+
+        def load_low(b, piece=0, pieces=1):
+            rows = SIDE // pieces
+            low_raw[b, piece] = raw.tile([P, PACK, rows * ROW_PAIR], BF16, name="low_raw")
+            cols = slice(piece * rows * ROW_PAIR, (piece + 1) * rows * ROW_PAIR)
+            channels = fmap_low[b].rearrange("(p t) y x -> p t (y x)", t=PACK)
+            nc.sync.dma_start(out=low_raw[b, piece][:], in_=channels[:, :, cols])
 
         def regroup_high(b, g):
             if g == 0:
@@ -103,18 +114,22 @@ def tile_avsl_graph_pa_kernel(tc, fmap_low, w_low, fmap_high, w_high, out):
                 in_=high_raw[b][:, g].rearrange("p t (c i) -> p c t i", i=RUN),
             )
 
-        def regroup_low(b):
+        def regroup_low(b, pieces=1):
             low_grouped[b] = grouped.tile([P, N_WIN, N_POS, PACK], BF16, name="low_grouped", align_bytes=64)
-            source = low_raw[b][:].rearrange(
-                "p t (yy dy xx dx) -> p dy yy xx t dx", dy=WIN, xx=SIDE, dx=WIN
-            )
             target = low_grouped[b][:].rearrange(
                 "p (dy dx) (yy xx) t -> p dy yy xx t dx", dy=WIN, xx=SIDE
             )
-            for dy in range(WIN):
-                nc.vector.tensor_copy(out=target[:, dy], in_=source[:, dy])
+            rows = SIDE // pieces
+            for piece in range(pieces):
+                source = low_raw[b, piece][:].rearrange(
+                    "p t (yy dy xx dx) -> p dy yy xx t dx", dy=WIN, xx=SIDE, dx=WIN
+                )
+                for dy in range(WIN):
+                    nc.vector.tensor_copy(
+                        out=target[:, dy, piece * rows : (piece + 1) * rows], in_=source[:, dy]
+                    )
 
-        def quantise(b):
+        def quantise_high(b):
             high_codes[b] = quantised.tile([P, HIGH_PASSES * N_POS], U32, name="high_codes", align_bytes=64)
             high_scales[b] = quantised.tile([P, HIGH_PASSES * N_POS], U8, name="high_scales", align_bytes=64)
             nc.vector.quantize_mx(
@@ -122,20 +137,33 @@ def tile_avsl_graph_pa_kernel(tc, fmap_low, w_low, fmap_high, w_high, out):
                 scales=high_scales[b][:],
                 in_=high_grouped[b][:].rearrange("p g i t -> p (g i t)"),
             )
-            low_codes[b] = quantised.tile([P, N_LOW], U32, name="low_codes", align_bytes=64)
-            low_scales[b] = quantised.tile([P, N_LOW], U8, name="low_scales", align_bytes=64)
+
+        def quantise_low(b, first=0, count=N_WIN):
+            if first == 0:
+                low_codes[b] = quantised.tile([P, N_LOW], U32, name="low_codes", align_bytes=64)
+                low_scales[b] = quantised.tile([P, N_LOW], U8, name="low_scales", align_bytes=64)
+            cols = slice(first * N_POS, (first + count) * N_POS)
             nc.vector.quantize_mx(
-                out=low_codes[b][:].bitcast(FP8X4),
-                scales=low_scales[b][:],
-                in_=low_grouped[b][:].rearrange("p w i t -> p (w i t)"),
+                out=low_codes[b][:, cols].bitcast(FP8X4),
+                scales=low_scales[b][:, cols],
+                in_=low_grouped[b][:, first : first + count].rearrange("p w i t -> p (w i t)"),
             )
 
-        def multiply(b):
-            cam[b] = psum_cam.tile([P, LEVELS, N_POS], F32, name="cam")
+        def open_cam(b):
+            if b < BATCH - 1:
+                both = psum_cam.tile([P, LEVELS, N_POS], F32, name="cam")
+                for level in range(LEVELS):
+                    cam[b, level] = both[:, level, :]
+            else:
+                for level in range(LEVELS):
+                    alone = psum_cam.tile([P, N_POS], F32, name="alone", tag="cam")
+                    cam[b, level] = alone[:]
+
+        def multiply_high(b):
             for g in range(HIGH_PASSES):
                 cols = slice(g * N_POS, (g + 1) * N_POS)
                 nc.tensor.matmul_mx(
-                    out=cam[b][:, 1, :],
+                    out=cam[b, 1],
                     lhsT=w_codes[:, 1 + g, :].bitcast(FP8X4),
                     lhsT_scale=w_scales[:, 1 + g, :],
                     rhs=high_codes[b][:, cols].bitcast(FP8X4),
@@ -143,10 +171,12 @@ def tile_avsl_graph_pa_kernel(tc, fmap_low, w_low, fmap_high, w_high, out):
                     start=(g == 0),
                     stop=(g == HIGH_PASSES - 1),
                 )
-            for w in range(N_WIN):
+
+        def multiply_low(b, first=0, count=N_WIN):
+            for w in range(first, first + count):
                 cols = slice(w * N_POS, (w + 1) * N_POS)
                 nc.tensor.matmul_mx(
-                    out=cam[b][:, 0, :],
+                    out=cam[b, 0],
                     lhsT=w_codes[:, 0, :].bitcast(FP8X4),
                     lhsT_scale=w_scales[:, 0, :],
                     rhs=low_codes[b][:, cols].bitcast(FP8X4),
@@ -155,70 +185,85 @@ def tile_avsl_graph_pa_kernel(tc, fmap_low, w_low, fmap_high, w_high, out):
                     stop=(w == N_WIN - 1),
                 )
 
-        def sum_squares(b):
+        def sum_squares(b, levels=BOTH):
             j, e = divmod(b, PAIR)
-            if e == 0:
+            if j not in sumsq:
                 sumsq[j] = small.tile([P, PAIR, LEVELS], F32, name="sumsq")
-            for level in range(LEVELS):
+                clamped[j] = small.tile([P, PAIR, LEVELS], F32, name="clamped")
+                inverse_norm[j] = small.tile([P, PAIR, LEVELS], F32, name="inverse_norm")
+            for level in levels:
                 squares = scratch.tile([P, N_POS], BF16, name="squares")
                 nc.scalar.activation(
                     out=squares[:],
-                    in_=cam[b][:, level, :],
+                    in_=cam[b, level],
                     func=ACT.Square,
                     scale=TO_MEAN[level],
                     accum_out=sumsq[j][:, e, level : level + 1],
                 )
 
-        def clamp_squares(j):
-            clamped[j] = small.tile([P, PAIR, LEVELS], F32, name="clamped")
-            nc.scalar.activation(out=clamped[j][:], in_=sumsq[j][:], func=ACT.Relu, bias=-(EPS**2))
+        def span(part):
+            return slice(part[0], part[-1] + 1)
 
-        def invert_norms(j):
-            inverse_norm[j] = small.tile([P, PAIR, LEVELS], F32, name="inverse_norm")
+        def clamp_squares(j, samples=BOTH, levels=BOTH):
             nc.scalar.activation(
-                out=inverse_norm[j][:], in_=clamped[j][:], func=ACT.Abs_reciprocal_sqrt, bias=EPS**2
+                out=clamped[j][:, span(samples), span(levels)],
+                in_=sumsq[j][:, span(samples), span(levels)],
+                func=ACT.Relu,
+                bias=-(EPS**2),
             )
 
-        def normalise_and_turn(j):
-            for level in range(LEVELS):
-                unit_sorted[j, level] = grouped.tile([P, PACK, P], BF16, name="unit_sorted")
-            for e in range(PAIR):
-                for level in range(LEVELS):
+        def invert_norms(j, samples=BOTH, levels=BOTH):
+            nc.scalar.activation(
+                out=inverse_norm[j][:, span(samples), span(levels)],
+                in_=clamped[j][:, span(samples), span(levels)],
+                func=ACT.Abs_reciprocal_sqrt,
+                bias=EPS**2,
+            )
+
+        def normalise(j, samples=BOTH, levels=BOTH):
+            for e in samples:
+                for level in levels:
+                    if (j, level) not in unit:
+                        unit[j, level] = grouped.tile([P, K_PASS], BF16, name="unit")
                     nc.scalar.activation(
-                        out=unit_sorted[j, level][:, :, e * P_SAMPLE : (e + 1) * P_SAMPLE],
-                        in_=cam[PAIR * j + e][:, level, :].rearrange("r (p t) -> r t p", t=PACK),
+                        out=unit[j, level][:, e * N_POS : (e + 1) * N_POS],
+                        in_=cam[PAIR * j + e, level],
                         func=ACT.Copy,
                         scale=inverse_norm[j][:, e, level : level + 1],
                     )
-            for level in range(LEVELS):
-                unit_turned[j, level] = psum_turn.tile([P, PACK, P], BF16, name="unit_turned", tag="turned")
-                for t in range(PACK):
-                    nc.tensor.transpose(unit_turned[j, level][:, t, :], unit_sorted[j, level][:, t, :], identity[:])
 
-        def regroup_unit(j):
-            unit_grouped[j] = grouped.tile([P, LEVELS, P, PACK], BF16, name="unit_grouped", align_bytes=64)
-            for level in range(LEVELS):
-                nc.scalar.activation(
-                    out=unit_grouped[j][:, level],
-                    in_=unit_turned[j, level][:].rearrange("p t r -> p r t"),
-                    func=ACT.Copy,
-                    scale=TO_MEAN[level],
-                )
+        def turn(j, levels=BOTH):
+            unit_turned[j, levels] = psum_turn.tile([P, len(levels), WORDS, P], F32, name="unit_turned", tag="turned")
+            for at, level in enumerate(levels):
+                words = unit[j, level][:].bitcast(F32)
+                for u in range(WORDS):
+                    nc.tensor.transpose(unit_turned[j, levels][:, at, u, :], words[:, u::WORDS], identity_words[:])
+
+        def regroup_unit(j, levels=BOTH):
+            if j not in unit_grouped:
+                unit_grouped[j] = grouped.tile([P, LEVELS, P, PACK], BF16, name="unit_grouped", align_bytes=64)
+            nc.scalar.copy(
+                out=unit_grouped[j][:, span(levels)].rearrange("p l r t -> p (l r t)").bitcast(F32),
+                in_=unit_turned[j, levels][:].rearrange("p l u r -> p l r u"),
+            )
+
+        def quantise_unit(j, levels=BOTH):
+            if j not in unit_codes:
+                unit_codes[j] = quantised.tile([P, LEVELS, P], U32, name="unit_codes", align_bytes=64)
+                unit_scales[j] = quantised.tile([P, LEVELS, P], U8, name="unit_scales", align_bytes=64)
+            nc.vector.quantize_mx(
+                out=unit_codes[j][:, span(levels)].rearrange("p l r -> p (l r)").bitcast(FP8X4),
+                scales=unit_scales[j][:, span(levels)].rearrange("p l r -> p (l r)"),
+                in_=unit_grouped[j][:, span(levels)].rearrange("p l r t -> p (l r t)"),
+            )
 
         def link_pass(j):
-            unit_codes = quantised.tile([P, LEVELS * P], U32, name="unit_codes", align_bytes=64)
-            unit_scales = quantised.tile([P, LEVELS * P], U8, name="unit_scales", align_bytes=64)
-            nc.vector.quantize_mx(
-                out=unit_codes[:].bitcast(FP8X4),
-                scales=unit_scales[:],
-                in_=unit_grouped[j][:].rearrange("p l r t -> p (l r t)"),
-            )
             nc.tensor.matmul_mx(
                 out=link[:],
-                lhsT=unit_codes[:, 0:P].bitcast(FP8X4),
-                lhsT_scale=unit_scales[:, 0:P],
-                rhs=unit_codes[:, P:].bitcast(FP8X4),
-                rhs_scale=unit_scales[:, P:],
+                lhsT=unit_codes[j][:, 0, :].bitcast(FP8X4),
+                lhsT_scale=unit_scales[j][:, 0, :],
+                rhs=unit_codes[j][:, 1, :].bitcast(FP8X4),
+                rhs_scale=unit_scales[j][:, 1, :],
                 start=(j == 0),
                 stop=(j == PAIRS - 1),
             )
@@ -227,42 +272,91 @@ def tile_avsl_graph_pa_kernel(tc, fmap_low, w_low, fmap_high, w_high, out):
             j, odd = divmod(step - lag, PAIR)
             return j if odd == 0 and 0 <= j < PAIRS else None
 
-        load(0)
+        load_low(0, 0, 2)
+        load_high(0, 0, 1)
+        load_low(0, 1, 2)
+        load_high(0, 1, 1)
         load_weights()
+        load_low(1)
+        load_high(1)
+        regroup_low(0, 2)
         regroup_high(0, 0)
         regroup_high(0, 1)
-        regroup_low(0)
         turn_weights()
-        for step in range(BATCH + 3):
+        quantise_low(0)
+        quantise_high(0)
+        regroup_low(1)
+        quantise_weights()
+        quantise_low(1)
+        open_cam(0)
+        multiply_high(0)
+        multiply_low(0)
+        regroup_high(1, 0)
+        regroup_high(1, 1)
+
+        last = BATCH - 1
+        for step in range(1, last):
             normed = pair_at(step, 2)
             linked = pair_at(step, 4)
             turned = pair_at(step, 3)
-            if 1 <= step <= BATCH:
-                sum_squares(step - 1)
-            if step + 1 < BATCH:
-                load(step + 1)
-                regroup_high(step + 1, 0)
+            sum_squares(step - 1)
+            load_high(step + 1)
+            load_low(step + 1)
+            regroup_high(step + 1, 0)
             if normed is not None:
                 clamp_squares(normed)
-            if step + 1 < BATCH:
-                regroup_high(step + 1, 1)
+            regroup_high(step + 1, 1)
             if normed is not None:
                 invert_norms(normed)
-            if step < BATCH:
-                quantise(step)
-            if step == 0:
-                quantise_weights()
-            if step < BATCH:
-                multiply(step)
+            quantise_high(step)
+            if step > 1:
+                quantise_low(step)
+            open_cam(step)
+            multiply_high(step)
+            multiply_low(step)
             if linked is not None:
+                quantise_unit(linked)
                 link_pass(linked)
-            if step + 1 < BATCH:
-                regroup_low(step + 1)
+            regroup_low(step + 1)
             if normed is not None:
-                normalise_and_turn(normed)
+                normalise(normed)
+                turn(normed)
             if turned is not None:
                 regroup_unit(turned)
 
+        even, odd = (0,), (1,)
+        low, high = (0,), (1,)
+        j = PAIRS - 1
+        sum_squares(last - 1)
+        clamp_squares(j, even)
+        regroup_unit(j - 1)
+        invert_norms(j, even)
+        quantise_high(last)
+        open_cam(last)
+        multiply_high(last)
+        for w in range(N_WIN):
+            quantise_low(last, w, 1)
+            multiply_low(last, w, 1)
+        quantise_unit(j - 1)
+        link_pass(j - 1)
+        sum_squares(last, high)
+        normalise(j, even, low)
+        clamp_squares(j, odd, high)
+        normalise(j, even, high)
+        invert_norms(j, odd, high)
+        normalise(j, odd, high)
+        turn(j, high)
+        sum_squares(last, low)
+        clamp_squares(j, odd, low)
+        invert_norms(j, odd, low)
+        normalise(j, odd, low)
+        turn(j, low)
+        regroup_unit(j, high)
+        regroup_unit(j, low)
+        quantise_unit(j, high)
+        quantise_unit(j, low)
+        link_pass(j)
+
         result = consts.tile([P, P], F32, name="result")
-        nc.scalar.activation(out=result[:], in_=link[:], func=ACT.Copy, scale=1.0 / BATCH)
+        nc.scalar.activation(out=result[:], in_=link[:], func=ACT.Copy, scale=TO_MEAN[0] / BATCH)
         nc.sync.dma_start(out=out, in_=result[:])

@@ -24,6 +24,7 @@ N_LOW = N_POS * N_WIN
 ROW_PAIR = N_LOW // SIDE
 HIGH_PASSES = C_HIGH // K_PASS
 W_PASSES = C_LOW // K_PASS + HIGH_PASSES
+LIFTED = 64
 LEVELS = 2
 BOTH = (0, 1)
 WORDS = 2
@@ -47,7 +48,8 @@ def tile_avsl_graph_pa_kernel(tc, fmap_low, w_low, fmap_high, w_high, out):
         scratch = ctx.enter_context(tc.tile_pool(name="scratch", bufs=4))
         small = ctx.enter_context(tc.tile_pool(name="small", bufs=3))
         psum_cam = ctx.enter_context(tc.psum_pool(name="psum_cam", bufs=3))
-        psum_turn = ctx.enter_context(tc.psum_pool(name="psum_turn", bufs=4))
+        psum_turn = ctx.enter_context(tc.psum_pool(name="psum_turn", bufs=2))
+        psum_lift = ctx.enter_context(tc.psum_pool(name="psum_lift", bufs=2))
         psum_link = ctx.enter_context(tc.psum_pool(name="psum_link", bufs=1))
 
         identity = consts.tile([P, P], BF16, name="identity")
@@ -86,7 +88,7 @@ def tile_avsl_graph_pa_kernel(tc, fmap_low, w_low, fmap_high, w_high, out):
         low_raw, high_raw, low_grouped, high_grouped = {}, {}, {}, {}
         low_codes, low_scales, high_codes, high_scales = {}, {}, {}, {}
         cam, sumsq, clamped, inverse_norm, unit, unit_turned, unit_grouped = {}, {}, {}, {}, {}, {}, {}
-        unit_codes, unit_scales = {}, {}
+        unit_codes, unit_scales, lifted = {}, {}, {}
         link = psum_link.tile([P, P], F32, name="link")
 
         def load_high(b, first=0, count=HIGH_PASSES):
@@ -104,14 +106,28 @@ def tile_avsl_graph_pa_kernel(tc, fmap_low, w_low, fmap_high, w_high, out):
             channels = fmap_low[b].rearrange("(p t) y x -> p t (y x)", t=PACK)
             nc.sync.dma_start(out=low_raw[b, piece][:], in_=channels[:, :, cols])
 
-        def regroup_high(b, g):
-            if g == 0:
+        def lift(b):
+            lifted[b] = psum_lift.tile([P, HIGH_PASSES, LIFTED, PACK], BF16, name="lifted")
+            nc.tensor.matmul(
+                lifted[b][:].rearrange("p g i t -> p g t i"),
+                lhsT=identity[:],
+                rhs=high_raw[b][:, :, :, N_POS - LIFTED :],
+                start=True,
+                stop=True,
+            )
+
+        def settle(b):
+            nc.scalar.copy(out=high_grouped[b][:, :, N_POS - LIFTED :, :], in_=lifted[b][:])
+
+        def regroup_high(b, first=0, count=HIGH_PASSES):
+            if first == 0:
                 high_grouped[b] = grouped.tile(
                     [P, HIGH_PASSES, N_POS, PACK], BF16, name="high_grouped", align_bytes=64
                 )
+            passes = slice(first, first + count)
             nc.scalar.copy(
-                out=high_grouped[b][:, g].rearrange("p (c i) t -> p c t i", i=RUN),
-                in_=high_raw[b][:, g].rearrange("p t (c i) -> p c t i", i=RUN),
+                out=high_grouped[b][:, passes, : N_POS - LIFTED].rearrange("p g (c i) t -> p g c t i", i=RUN),
+                in_=high_raw[b][:, passes, :, : N_POS - LIFTED].rearrange("p g t (c i) -> p g c t i", i=RUN),
             )
 
         def regroup_low(b, pieces=1):
@@ -280,9 +296,12 @@ def tile_avsl_graph_pa_kernel(tc, fmap_low, w_low, fmap_high, w_high, out):
         load_low(1)
         load_high(1)
         regroup_low(0, 2)
-        regroup_high(0, 0)
-        regroup_high(0, 1)
+        lift(0)
+        regroup_high(0, 0, 1)
+        regroup_high(0, 1, 1)
+        settle(0)
         turn_weights()
+        lift(1)
         quantise_low(0)
         quantise_high(0)
         regroup_low(1)
@@ -291,8 +310,8 @@ def tile_avsl_graph_pa_kernel(tc, fmap_low, w_low, fmap_high, w_high, out):
         open_cam(0)
         multiply_high(0)
         multiply_low(0)
-        regroup_high(1, 0)
-        regroup_high(1, 1)
+        regroup_high(1)
+        settle(1)
 
         last = BATCH - 1
         for step in range(1, last):
@@ -302,12 +321,13 @@ def tile_avsl_graph_pa_kernel(tc, fmap_low, w_low, fmap_high, w_high, out):
             sum_squares(step - 1)
             load_high(step + 1)
             load_low(step + 1)
-            regroup_high(step + 1, 0)
+            lift(step + 1)
             if normed is not None:
                 clamp_squares(normed)
-            regroup_high(step + 1, 1)
+            regroup_high(step + 1)
             if normed is not None:
                 invert_norms(normed)
+            settle(step + 1)
             quantise_high(step)
             if step > 1:
                 quantise_low(step)

@@ -24,6 +24,7 @@ N_LOW = N_POS * N_WIN
 ROW_PAIR = N_LOW // SIDE
 HIGH_PASSES = C_HIGH // K_PASS
 W_PASSES = C_LOW // K_PASS + HIGH_PASSES
+SHARE = 2
 LIFTED = 64
 LEVELS = 2
 BOTH = (0, 1)
@@ -107,6 +108,7 @@ def tile_avsl_graph_pa_kernel(tc, fmap_low, w_low, fmap_high, w_high, out):
             nc.sync.dma_start(out=low_raw[b, piece][:], in_=channels[:, :, cols])
 
         def lift(b):
+            high_grouped[b] = grouped.tile([P, HIGH_PASSES, N_POS, PACK], BF16, name="high_grouped", align_bytes=64)
             lifted[b] = psum_lift.tile([P, HIGH_PASSES, LIFTED, PACK], BF16, name="lifted")
             nc.tensor.matmul(
                 lifted[b][:].rearrange("p g i t -> p g t i"),
@@ -120,30 +122,31 @@ def tile_avsl_graph_pa_kernel(tc, fmap_low, w_low, fmap_high, w_high, out):
             nc.scalar.copy(out=high_grouped[b][:, :, N_POS - LIFTED :, :], in_=lifted[b][:])
 
         def regroup_high(b, first=0, count=HIGH_PASSES):
-            if first == 0:
-                high_grouped[b] = grouped.tile(
-                    [P, HIGH_PASSES, N_POS, PACK], BF16, name="high_grouped", align_bytes=64
-                )
             passes = slice(first, first + count)
             nc.scalar.copy(
                 out=high_grouped[b][:, passes, : N_POS - LIFTED].rearrange("p g (c i) t -> p g c t i", i=RUN),
                 in_=high_raw[b][:, passes, :, : N_POS - LIFTED].rearrange("p g t (c i) -> p g c t i", i=RUN),
             )
 
-        def regroup_low(b, pieces=1):
-            low_grouped[b] = grouped.tile([P, N_WIN, N_POS, PACK], BF16, name="low_grouped", align_bytes=64)
-            target = low_grouped[b][:].rearrange(
-                "p (dy dx) (yy xx) t -> p dy yy xx t dx", dy=WIN, xx=SIDE
-            )
+        def low_views(b, piece, pieces):
             rows = SIDE // pieces
+            source = low_raw[b, piece][:].rearrange(
+                "p t (yy dy xx dx) -> p yy dy xx t dx", dy=WIN, xx=SIDE, dx=WIN
+            )
+            target = low_grouped[b][:].rearrange("p (dy dx) (yy xx) t -> p yy dy xx t dx", dy=WIN, xx=SIDE)
+            return target[:, piece * rows : (piece + 1) * rows], source
+
+        def open_low(b):
+            low_grouped[b] = grouped.tile([P, N_WIN, N_POS, PACK], BF16, name="low_grouped", align_bytes=64)
+
+        def share_low(b):
+            target, source = low_views(b, 0, 1)
+            nc.scalar.copy(out=target[:, :, :, SIDE - SHARE :], in_=source[:, :, :, SIDE - SHARE :])
+
+        def regroup_low(b, pieces=1, columns=SIDE):
             for piece in range(pieces):
-                source = low_raw[b, piece][:].rearrange(
-                    "p t (yy dy xx dx) -> p dy yy xx t dx", dy=WIN, xx=SIDE, dx=WIN
-                )
-                for dy in range(WIN):
-                    nc.vector.tensor_copy(
-                        out=target[:, dy, piece * rows : (piece + 1) * rows], in_=source[:, dy]
-                    )
+                target, source = low_views(b, piece, pieces)
+                nc.vector.tensor_copy(out=target[:, :, :, :columns], in_=source[:, :, :, :columns])
 
         def quantise_high(b):
             high_codes[b] = quantised.tile([P, HIGH_PASSES * N_POS], U32, name="high_codes", align_bytes=64)
@@ -236,17 +239,17 @@ def tile_avsl_graph_pa_kernel(tc, fmap_low, w_low, fmap_high, w_high, out):
                 bias=EPS**2,
             )
 
-        def normalise(j, samples=BOTH, levels=BOTH):
+        def normalise(j, samples=BOTH, levels=BOTH, on_vector=False):
             for e in samples:
                 for level in levels:
                     if (j, level) not in unit:
                         unit[j, level] = grouped.tile([P, K_PASS], BF16, name="unit")
-                    nc.scalar.activation(
-                        out=unit[j, level][:, e * N_POS : (e + 1) * N_POS],
-                        in_=cam[PAIR * j + e, level],
-                        func=ACT.Copy,
-                        scale=inverse_norm[j][:, e, level : level + 1],
-                    )
+                    columns = unit[j, level][:, e * N_POS : (e + 1) * N_POS]
+                    factor = inverse_norm[j][:, e, level : level + 1]
+                    if on_vector:
+                        nc.vector.tensor_scalar_mul(columns, cam[PAIR * j + e, level], factor)
+                    else:
+                        nc.scalar.activation(out=columns, in_=cam[PAIR * j + e, level], func=ACT.Copy, scale=factor)
 
         def turn(j, levels=BOTH):
             unit_turned[j, levels] = psum_turn.tile([P, len(levels), WORDS, P], F32, name="unit_turned", tag="turned")
@@ -255,10 +258,11 @@ def tile_avsl_graph_pa_kernel(tc, fmap_low, w_low, fmap_high, w_high, out):
                 for u in range(WORDS):
                     nc.tensor.transpose(unit_turned[j, levels][:, at, u, :], words[:, u::WORDS], identity_words[:])
 
-        def regroup_unit(j, levels=BOTH):
+        def regroup_unit(j, levels=BOTH, on_vector=False):
             if j not in unit_grouped:
                 unit_grouped[j] = grouped.tile([P, LEVELS, P, PACK], BF16, name="unit_grouped", align_bytes=64)
-            nc.scalar.copy(
+            copy = nc.vector.tensor_copy if on_vector else nc.scalar.copy
+            copy(
                 out=unit_grouped[j][:, span(levels)].rearrange("p l r t -> p (l r t)").bitcast(F32),
                 in_=unit_turned[j, levels][:].rearrange("p l u r -> p l r u"),
             )
@@ -295,6 +299,7 @@ def tile_avsl_graph_pa_kernel(tc, fmap_low, w_low, fmap_high, w_high, out):
         load_weights()
         load_low(1)
         load_high(1)
+        open_low(0)
         regroup_low(0, 2)
         lift(0)
         regroup_high(0, 0, 1)
@@ -304,8 +309,9 @@ def tile_avsl_graph_pa_kernel(tc, fmap_low, w_low, fmap_high, w_high, out):
         lift(1)
         quantise_low(0)
         quantise_high(0)
-        regroup_low(1)
         quantise_weights()
+        open_low(1)
+        regroup_low(1)
         quantise_low(1)
         open_cam(0)
         multiply_high(0)
@@ -316,18 +322,22 @@ def tile_avsl_graph_pa_kernel(tc, fmap_low, w_low, fmap_high, w_high, out):
         last = BATCH - 1
         for step in range(1, last):
             normed = pair_at(step, 2)
-            linked = pair_at(step, 4)
-            turned = pair_at(step, 3)
+            turned = pair_at(step, 4)
+            linked = pair_at(step, 5)
             sum_squares(step - 1)
             load_high(step + 1)
             load_low(step + 1)
             lift(step + 1)
+            settle(step + 1)
+            open_low(step + 1)
+            shared = normed is None and step > 1
+            if shared:
+                share_low(step + 1)
             if normed is not None:
                 clamp_squares(normed)
             regroup_high(step + 1)
             if normed is not None:
                 invert_norms(normed)
-            settle(step + 1)
             quantise_high(step)
             if step > 1:
                 quantise_low(step)
@@ -337,41 +347,40 @@ def tile_avsl_graph_pa_kernel(tc, fmap_low, w_low, fmap_high, w_high, out):
             if linked is not None:
                 quantise_unit(linked)
                 link_pass(linked)
-            regroup_low(step + 1)
+            regroup_low(step + 1, columns=SIDE - SHARE if shared else SIDE)
+            if turned is not None:
+                regroup_unit(turned)
             if normed is not None:
                 normalise(normed)
                 turn(normed)
-            if turned is not None:
-                regroup_unit(turned)
 
         even, odd = (0,), (1,)
         low, high = (0,), (1,)
         j = PAIRS - 1
         sum_squares(last - 1)
-        clamp_squares(j, even)
-        regroup_unit(j - 1)
-        invert_norms(j, even)
         quantise_high(last)
         open_cam(last)
         multiply_high(last)
+        clamp_squares(j, even)
+        sum_squares(last, high)
+        invert_norms(j, even)
         for w in range(N_WIN):
             quantise_low(last, w, 1)
             multiply_low(last, w, 1)
-        quantise_unit(j - 1)
-        link_pass(j - 1)
-        sum_squares(last, high)
-        normalise(j, even, low)
-        clamp_squares(j, odd, high)
-        normalise(j, even, high)
-        invert_norms(j, odd, high)
-        normalise(j, odd, high)
-        turn(j, high)
+        quantise_unit(j - 2)
+        link_pass(j - 2)
+        regroup_unit(j - 1, on_vector=True)
+        normalise(j, even, on_vector=True)
         sum_squares(last, low)
-        clamp_squares(j, odd, low)
-        invert_norms(j, odd, low)
+        clamp_squares(j, odd)
+        invert_norms(j, odd)
+        normalise(j, odd, high, on_vector=True)
         normalise(j, odd, low)
+        quantise_unit(j - 1)
+        turn(j, high)
         turn(j, low)
-        regroup_unit(j, high)
+        link_pass(j - 1)
+        regroup_unit(j, high, on_vector=True)
         regroup_unit(j, low)
         quantise_unit(j, high)
         quantise_unit(j, low)

@@ -25,7 +25,7 @@ ROW_PAIR = N_LOW // SIDE
 HIGH_PASSES = C_HIGH // K_PASS
 W_PASSES = C_LOW // K_PASS + HIGH_PASSES
 SHARE = 2
-LIFTED = 64
+LIFTED = 76
 LEVELS = 2
 BOTH = (0, 1)
 WORDS = 2
@@ -44,7 +44,7 @@ def tile_avsl_graph_pa_kernel(tc, fmap_low, w_low, fmap_high, w_high, out):
         ctx.enter_context(tc.manual_schedule())
         consts = ctx.enter_context(tc.tile_pool(name="consts", bufs=1))
         raw = ctx.enter_context(tc.tile_pool(name="raw", bufs=6))
-        grouped = ctx.enter_context(tc.tile_pool(name="grouped", bufs=3))
+        grouped = ctx.enter_context(tc.tile_pool(name="grouped", bufs=4))
         quantised = ctx.enter_context(tc.tile_pool(name="quantised", bufs=3))
         scratch = ctx.enter_context(tc.tile_pool(name="scratch", bufs=4))
         small = ctx.enter_context(tc.tile_pool(name="small", bufs=3))
@@ -110,13 +110,14 @@ def tile_avsl_graph_pa_kernel(tc, fmap_low, w_low, fmap_high, w_high, out):
         def lift(b):
             high_grouped[b] = grouped.tile([P, HIGH_PASSES, N_POS, PACK], BF16, name="high_grouped", align_bytes=64)
             lifted[b] = psum_lift.tile([P, HIGH_PASSES, LIFTED, PACK], BF16, name="lifted")
-            nc.tensor.matmul(
-                lifted[b][:].rearrange("p g i t -> p g t i"),
-                lhsT=identity[:],
-                rhs=high_raw[b][:, :, :, N_POS - LIFTED :],
-                start=True,
-                stop=True,
-            )
+            for g in range(HIGH_PASSES):
+                nc.tensor.matmul(
+                    lifted[b][:, g].rearrange("p i t -> p t i"),
+                    lhsT=identity[:],
+                    rhs=high_raw[b][:, g, :, N_POS - LIFTED :],
+                    start=True,
+                    stop=True,
+                )
 
         def settle(b):
             nc.scalar.copy(out=high_grouped[b][:, :, N_POS - LIFTED :, :], in_=lifted[b][:])
@@ -297,8 +298,9 @@ def tile_avsl_graph_pa_kernel(tc, fmap_low, w_low, fmap_high, w_high, out):
         load_low(0, 1, 2)
         load_high(0, 1, 1)
         load_weights()
-        load_low(1)
-        load_high(1)
+        for b in (1, 2):
+            load_low(b)
+            load_high(b)
         open_low(0)
         regroup_low(0, 2)
         lift(0)
@@ -311,35 +313,37 @@ def tile_avsl_graph_pa_kernel(tc, fmap_low, w_low, fmap_high, w_high, out):
         quantise_high(0)
         quantise_weights()
         open_low(1)
-        regroup_low(1)
+        target, source = low_views(1, 0, 1)
+        lower, upper = slice(SIDE // 2, SIDE), slice(0, SIDE // 2)
+        nc.scalar.copy(out=target[:, lower, 1], in_=source[:, lower, 1])
+        nc.vector.tensor_copy(out=target[:, :, 0], in_=source[:, :, 0])
+        nc.vector.tensor_copy(out=target[:, upper, 1], in_=source[:, upper, 1])
         quantise_low(1)
         open_cam(0)
         multiply_high(0)
         multiply_low(0)
         regroup_high(1)
         settle(1)
+        lift(2)
 
         last = BATCH - 1
+        shared = set()
         for step in range(1, last):
             normed = pair_at(step, 2)
             turned = pair_at(step, 4)
             linked = pair_at(step, 5)
             sum_squares(step - 1)
-            load_high(step + 1)
-            load_low(step + 1)
-            lift(step + 1)
+            if step + 2 < BATCH:
+                load_high(step + 2)
+                load_low(step + 2)
             settle(step + 1)
-            open_low(step + 1)
-            shared = normed is None and step > 1
-            if shared:
-                share_low(step + 1)
             if normed is not None:
                 clamp_squares(normed)
             regroup_high(step + 1)
             if normed is not None:
                 invert_norms(normed)
             quantise_high(step)
-            if step > 1:
+            if step > 2:
                 quantise_low(step)
             open_cam(step)
             multiply_high(step)
@@ -347,12 +351,22 @@ def tile_avsl_graph_pa_kernel(tc, fmap_low, w_low, fmap_high, w_high, out):
             if linked is not None:
                 quantise_unit(linked)
                 link_pass(linked)
-            regroup_low(step + 1, columns=SIDE - SHARE if shared else SIDE)
+            if step + 1 not in shared:
+                open_low(step + 1)
+            regroup_low(step + 1, columns=SIDE - SHARE if step + 1 in shared else SIDE)
+            if step == 1:
+                quantise_low(step + 1)
+            if step + 2 < BATCH:
+                lift(step + 2)
             if turned is not None:
                 regroup_unit(turned)
             if normed is not None:
                 normalise(normed)
                 turn(normed)
+            elif 1 < step < last - 1:
+                open_low(step + 2)
+                share_low(step + 2)
+                shared.add(step + 2)
 
         even, odd = (0,), (1,)
         low, high = (0,), (1,)
@@ -364,25 +378,27 @@ def tile_avsl_graph_pa_kernel(tc, fmap_low, w_low, fmap_high, w_high, out):
         clamp_squares(j, even)
         sum_squares(last, high)
         invert_norms(j, even)
+        clamp_squares(j, odd, high)
         for w in range(N_WIN):
             quantise_low(last, w, 1)
             multiply_low(last, w, 1)
+        invert_norms(j, odd, high)
         quantise_unit(j - 2)
         link_pass(j - 2)
-        regroup_unit(j - 1, on_vector=True)
         normalise(j, even, on_vector=True)
-        sum_squares(last, low)
-        clamp_squares(j, odd)
-        invert_norms(j, odd)
         normalise(j, odd, high, on_vector=True)
-        normalise(j, odd, low)
-        quantise_unit(j - 1)
         turn(j, high)
-        turn(j, low)
-        link_pass(j - 1)
+        sum_squares(last, low)
+        clamp_squares(j, odd, low)
+        regroup_unit(j - 1, on_vector=True)
+        invert_norms(j, odd, low)
         regroup_unit(j, high, on_vector=True)
-        regroup_unit(j, low)
+        normalise(j, odd, low)
+        turn(j, low)
+        quantise_unit(j - 1)
+        link_pass(j - 1)
         quantise_unit(j, high)
+        regroup_unit(j, low)
         quantise_unit(j, low)
         link_pass(j)
 

@@ -25,13 +25,14 @@ ROW_PAIR = N_LOW // SIDE
 HIGH_PASSES = C_HIGH // K_PASS
 W_PASSES = C_LOW // K_PASS + HIGH_PASSES
 SHARE = 2
-LIFTED = 76
+LIFTED = 80
 LEVELS = 2
+LATE = 4
 BOTH = (0, 1)
 WORDS = 2
 PAIR = K_PASS // N_POS
 PAIRS = BATCH // PAIR
-RUN = 4
+RUN = 8
 EPS = 1e-12
 TO_MEAN = (1.0 / N_WIN, 1.0)
 
@@ -46,6 +47,7 @@ def tile_avsl_graph_pa_kernel(tc, fmap_low, w_low, fmap_high, w_high, out):
         raw = ctx.enter_context(tc.tile_pool(name="raw", bufs=6))
         grouped = ctx.enter_context(tc.tile_pool(name="grouped", bufs=4))
         quantised = ctx.enter_context(tc.tile_pool(name="quantised", bufs=3))
+        units = ctx.enter_context(tc.tile_pool(name="units", bufs=LATE + 1))
         scratch = ctx.enter_context(tc.tile_pool(name="scratch", bufs=4))
         small = ctx.enter_context(tc.tile_pool(name="small", bufs=3))
         psum_cam = ctx.enter_context(tc.psum_pool(name="psum_cam", bufs=3))
@@ -261,7 +263,7 @@ def tile_avsl_graph_pa_kernel(tc, fmap_low, w_low, fmap_high, w_high, out):
 
         def regroup_unit(j, levels=BOTH, on_vector=False):
             if j not in unit_grouped:
-                unit_grouped[j] = grouped.tile([P, LEVELS, P, PACK], BF16, name="unit_grouped", align_bytes=64)
+                unit_grouped[j] = units.tile([P, LEVELS, P, PACK], BF16, name="unit_grouped", align_bytes=64)
             copy = nc.vector.tensor_copy if on_vector else nc.scalar.copy
             copy(
                 out=unit_grouped[j][:, span(levels)].rearrange("p l r t -> p (l r t)").bitcast(F32),
@@ -270,8 +272,8 @@ def tile_avsl_graph_pa_kernel(tc, fmap_low, w_low, fmap_high, w_high, out):
 
         def quantise_unit(j, levels=BOTH):
             if j not in unit_codes:
-                unit_codes[j] = quantised.tile([P, LEVELS, P], U32, name="unit_codes", align_bytes=64)
-                unit_scales[j] = quantised.tile([P, LEVELS, P], U8, name="unit_scales", align_bytes=64)
+                unit_codes[j] = units.tile([P, LEVELS, P], U32, name="unit_codes", align_bytes=64)
+                unit_scales[j] = units.tile([P, LEVELS, P], U8, name="unit_scales", align_bytes=64)
             nc.vector.quantize_mx(
                 out=unit_codes[j][:, span(levels)].rearrange("p l r -> p (l r)").bitcast(FP8X4),
                 scales=unit_scales[j][:, span(levels)].rearrange("p l r -> p (l r)"),
@@ -348,7 +350,7 @@ def tile_avsl_graph_pa_kernel(tc, fmap_low, w_low, fmap_high, w_high, out):
             open_cam(step)
             multiply_high(step)
             multiply_low(step)
-            if linked is not None:
+            if linked is not None and linked < PAIRS - LATE:
                 quantise_unit(linked)
                 link_pass(linked)
             if step + 1 not in shared:
@@ -383,8 +385,9 @@ def tile_avsl_graph_pa_kernel(tc, fmap_low, w_low, fmap_high, w_high, out):
             quantise_low(last, w, 1)
             multiply_low(last, w, 1)
         invert_norms(j, odd, high)
-        quantise_unit(j - 2)
-        link_pass(j - 2)
+        for late in range(PAIRS - LATE, j - 1):
+            quantise_unit(late)
+            link_pass(late)
         normalise(j, even, on_vector=True)
         normalise(j, odd, high, on_vector=True)
         turn(j, high)

from contextlib import ExitStack

import concourse.masks as masks
import concourse.mybir as mybir

F32 = mybir.dt.float32
BF16 = mybir.dt.bfloat16
U32 = mybir.dt.uint32
U8 = mybir.dt.uint8
FP8X4 = mybir.dt.float8_e4m3fn_x4
ACT = mybir.ActivationFunctionType

P = 128
PACK = 4
K_PASS = P * PACK
BATCH = 20
C_LOW = 512
C_HIGH = 1024
SIDE = 16
WIN = 2
N_POS = SIDE * SIDE
N_WIN = WIN * WIN
N_LOW = N_POS * N_WIN
ROW_PAIR = N_LOW // SIDE
HIGH_PASSES = C_HIGH // K_PASS
W_PASSES = C_LOW // K_PASS + HIGH_PASSES
SHARE = 2
LIFTED = 80
LEVELS = 2
LATE = 4
BOTH = (0, 1)
WORDS = 2
PAIR = K_PASS // N_POS
PAIRS = BATCH // PAIR
RUN = 8
EPS = 1e-12
TO_MEAN = (1.0 / N_WIN, 1.0)

FLOPS = 2 * P * BATCH * (C_LOW * N_LOW + C_HIGH * N_POS) + 2 * P * P * BATCH * N_POS


def tile_avsl_graph_pa_kernel(tc, fmap_low, w_low, fmap_high, w_high, out):
    nc = tc.nc
    with ExitStack() as ctx:
        ctx.enter_context(tc.manual_schedule())
        consts = ctx.enter_context(tc.tile_pool(name="consts", bufs=1))
        raw = ctx.enter_context(tc.tile_pool(name="raw", bufs=6))
        grouped = ctx.enter_context(tc.tile_pool(name="grouped", bufs=4))
        quantised = ctx.enter_context(tc.tile_pool(name="quantised", bufs=3))
        units = ctx.enter_context(tc.tile_pool(name="units", bufs=LATE + 1))
        scratch = ctx.enter_context(tc.tile_pool(name="scratch", bufs=4))
        small = ctx.enter_context(tc.tile_pool(name="small", bufs=3))
        psum_cam = ctx.enter_context(tc.psum_pool(name="psum_cam", bufs=3))
        psum_turn = ctx.enter_context(tc.psum_pool(name="psum_turn", bufs=2))
        psum_lift = ctx.enter_context(tc.psum_pool(name="psum_lift", bufs=2))
        psum_link = ctx.enter_context(tc.psum_pool(name="psum_link", bufs=1))

        identity = consts.tile([P, P], BF16, name="identity")
        masks.make_identity(nc, identity[:])
        identity_words = consts.tile([P, P], F32, name="identity_words")
        masks.make_identity(nc, identity_words[:])
        ones = consts.tile([P, 1], F32, name="ones")
        nc.vector.memset(ones[:], 1.0)
        nc.scalar.activation(out=ones[:], in_=ones[:], func=ACT.Abs_reciprocal_sqrt)

        w_rows = consts.tile([P, W_PASSES * K_PASS], BF16, name="w_rows")
        w_grouped = consts.tile([P, W_PASSES, P, PACK], BF16, name="w_grouped", align_bytes=64)
        w_codes = consts.tile([P, W_PASSES, P], U32, name="w_codes", align_bytes=64)
        w_scales = consts.tile([P, W_PASSES, P], U8, name="w_scales", align_bytes=64)

        def load_weights():
            nc.sync.dma_start(out=w_rows[:, 0:C_LOW], in_=w_low)
            nc.sync.dma_start(out=w_rows[:, C_LOW:], in_=w_high)

        def turn_weights():
            w_by_t = w_rows[:].rearrange("r (g p t) -> r g t p", g=W_PASSES, t=PACK)
            for g in range(W_PASSES):
                w_turned = psum_turn.tile([P, PACK, P], BF16, name="w_turned", tag="turned")
                for t in range(PACK):
                    nc.tensor.transpose(w_turned[:, t, :], w_by_t[:, g, t, :], identity[:])
                nc.scalar.copy(out=w_grouped[:, g], in_=w_turned[:].rearrange("p t r -> p r t"))

        def quantise_weights():
            for g in range(W_PASSES):
                nc.vector.quantize_mx(
                    out=w_codes[:, g, :].bitcast(FP8X4),
                    scales=w_scales[:, g, :],
                    in_=w_grouped[:, g].rearrange("p r t -> p (r t)"),
                )

        low_raw, high_raw, low_grouped, high_grouped = {}, {}, {}, {}
        low_codes, low_scales, high_codes, high_scales = {}, {}, {}, {}
        cam, sumsq, clamped, inverse_norm, unit, unit_turned, unit_grouped = {}, {}, {}, {}, {}, {}, {}
        unit_codes, unit_scales, lifted = {}, {}, {}
        link = psum_link.tile([P, P], F32, name="link")

        def load_high(b, first=0, count=HIGH_PASSES):
            if first == 0:
                high_raw[b] = raw.tile([P, HIGH_PASSES, PACK, N_POS], BF16, name="high_raw")
            channels = fmap_high[b].rearrange("(g p t) y x -> p g t (y x)", g=HIGH_PASSES, t=PACK)
            nc.sync.dma_start(
                out=high_raw[b][:, first : first + count], in_=channels[:, first : first + count]
            )

        def load_low(b, piece=0, pieces=1):
            rows = SIDE // pieces
            low_raw[b, piece] = raw.tile([P, PACK, rows * ROW_PAIR], BF16, name="low_raw")
            cols = slice(piece * rows * ROW_PAIR, (piece + 1) * rows * ROW_PAIR)
            channels = fmap_low[b].rearrange("(p t) y x -> p t (y x)", t=PACK)
            nc.sync.dma_start(out=low_raw[b, piece][:], in_=channels[:, :, cols])

        def lift(b):
            high_grouped[b] = grouped.tile([P, HIGH_PASSES, N_POS, PACK], BF16, name="high_grouped", align_bytes=64)
            lifted[b] = psum_lift.tile([P, HIGH_PASSES, LIFTED, PACK], BF16, name="lifted")
            for g in range(HIGH_PASSES):
                nc.tensor.matmul(
                    lifted[b][:, g].rearrange("p i t -> p t i"),
                    lhsT=identity[:],
                    rhs=high_raw[b][:, g, :, N_POS - LIFTED :],
                    start=True,
                    stop=True,
                )

        def settle(b):
            nc.scalar.copy(out=high_grouped[b][:, :, N_POS - LIFTED :, :], in_=lifted[b][:])

        def regroup_high(b, first=0, count=HIGH_PASSES):
            passes = slice(first, first + count)
            nc.scalar.copy(
                out=high_grouped[b][:, passes, : N_POS - LIFTED].rearrange("p g (c i) t -> p g c t i", i=RUN),
                in_=high_raw[b][:, passes, :, : N_POS - LIFTED].rearrange("p g t (c i) -> p g c t i", i=RUN),
            )

        def low_views(b, piece, pieces):
            rows = SIDE // pieces
            source = low_raw[b, piece][:].rearrange(
                "p t (yy dy xx dx) -> p yy dy xx t dx", dy=WIN, xx=SIDE, dx=WIN
            )
            target = low_grouped[b][:].rearrange("p (dy dx) (yy xx) t -> p yy dy xx t dx", dy=WIN, xx=SIDE)
            return target[:, piece * rows : (piece + 1) * rows], source

        def open_low(b):
            low_grouped[b] = grouped.tile([P, N_WIN, N_POS, PACK], BF16, name="low_grouped", align_bytes=64)

        def share_low(b):
            target, source = low_views(b, 0, 1)
            nc.scalar.copy(out=target[:, :, :, SIDE - SHARE :], in_=source[:, :, :, SIDE - SHARE :])

        def regroup_low(b, pieces=1, columns=SIDE):
            for piece in range(pieces):
                target, source = low_views(b, piece, pieces)
                nc.vector.tensor_copy(out=target[:, :, :, :columns], in_=source[:, :, :, :columns])

        def quantise_high(b):
            high_codes[b] = quantised.tile([P, HIGH_PASSES * N_POS], U32, name="high_codes", align_bytes=64)
            high_scales[b] = quantised.tile([P, HIGH_PASSES * N_POS], U8, name="high_scales", align_bytes=64)
            nc.vector.quantize_mx(
                out=high_codes[b][:].bitcast(FP8X4),
                scales=high_scales[b][:],
                in_=high_grouped[b][:].rearrange("p g i t -> p (g i t)"),
            )

        def quantise_low(b, first=0, count=N_WIN):
            if first == 0:
                low_codes[b] = quantised.tile([P, N_LOW], U32, name="low_codes", align_bytes=64)
                low_scales[b] = quantised.tile([P, N_LOW], U8, name="low_scales", align_bytes=64)
            cols = slice(first * N_POS, (first + count) * N_POS)
            nc.vector.quantize_mx(
                out=low_codes[b][:, cols].bitcast(FP8X4),
                scales=low_scales[b][:, cols],
                in_=low_grouped[b][:, first : first + count].rearrange("p w i t -> p (w i t)"),
            )

        def open_cam(b):
            if b < BATCH - 1:
                both = psum_cam.tile([P, LEVELS, N_POS], F32, name="cam")
                for level in range(LEVELS):
                    cam[b, level] = both[:, level, :]
            else:
                for level in range(LEVELS):
                    alone = psum_cam.tile([P, N_POS], F32, name="alone", tag="cam")
                    cam[b, level] = alone[:]

        def multiply_high(b):
            for g in range(HIGH_PASSES):
                cols = slice(g * N_POS, (g + 1) * N_POS)
                nc.tensor.matmul_mx(
                    out=cam[b, 1],
                    lhsT=w_codes[:, 1 + g, :].bitcast(FP8X4),
                    lhsT_scale=w_scales[:, 1 + g, :],
                    rhs=high_codes[b][:, cols].bitcast(FP8X4),
                    rhs_scale=high_scales[b][:, cols],
                    start=(g == 0),
                    stop=(g == HIGH_PASSES - 1),
                )

        def multiply_low(b, first=0, count=N_WIN):
            for w in range(first, first + count):
                cols = slice(w * N_POS, (w + 1) * N_POS)
                nc.tensor.matmul_mx(
                    out=cam[b, 0],
                    lhsT=w_codes[:, 0, :].bitcast(FP8X4),
                    lhsT_scale=w_scales[:, 0, :],
                    rhs=low_codes[b][:, cols].bitcast(FP8X4),
                    rhs_scale=low_scales[b][:, cols],
                    start=(w == 0),
                    stop=(w == N_WIN - 1),
                )

        def sum_squares(b, levels=BOTH):
            j, e = divmod(b, PAIR)
            if j not in sumsq:
                sumsq[j] = small.tile([P, PAIR, LEVELS], F32, name="sumsq")
                clamped[j] = small.tile([P, PAIR, LEVELS], F32, name="clamped")
                inverse_norm[j] = small.tile([P, PAIR, LEVELS], F32, name="inverse_norm")
            for level in levels:
                squares = scratch.tile([P, N_POS], BF16, name="squares")
                nc.scalar.activation(
                    out=squares[:],
                    in_=cam[b, level],
                    func=ACT.Square,
                    scale=TO_MEAN[level],
                    accum_out=sumsq[j][:, e, level : level + 1],
                )

        def span(part):
            return slice(part[0], part[-1] + 1)

        def clamp_squares(j, samples=BOTH, levels=BOTH):
            nc.scalar.activation(
                out=clamped[j][:, span(samples), span(levels)],
                in_=sumsq[j][:, span(samples), span(levels)],
                func=ACT.Relu,
                bias=-(EPS**2),
            )

        def invert_norms(j, samples=BOTH, levels=BOTH):
            nc.scalar.activation(
                out=inverse_norm[j][:, span(samples), span(levels)],
                in_=clamped[j][:, span(samples), span(levels)],
                func=ACT.Abs_reciprocal_sqrt,
                bias=EPS**2,
            )

        def normalise(j, samples=BOTH, levels=BOTH, on_vector=False):
            for e in samples:
                for level in levels:
                    if (j, level) not in unit:
                        unit[j, level] = grouped.tile([P, K_PASS], BF16, name="unit")
                    columns = unit[j, level][:, e * N_POS : (e + 1) * N_POS]
                    factor = inverse_norm[j][:, e, level : level + 1]
                    if on_vector:
                        nc.vector.tensor_scalar_mul(columns, cam[PAIR * j + e, level], factor)
                    else:
                        nc.scalar.activation(out=columns, in_=cam[PAIR * j + e, level], func=ACT.Copy, scale=factor)

        def turn(j, levels=BOTH):
            unit_turned[j, levels] = psum_turn.tile([P, len(levels), WORDS, P], F32, name="unit_turned", tag="turned")
            for at, level in enumerate(levels):
                words = unit[j, level][:].bitcast(F32)
                for u in range(WORDS):
                    nc.tensor.transpose(unit_turned[j, levels][:, at, u, :], words[:, u::WORDS], identity_words[:])

        def regroup_unit(j, levels=BOTH, on_vector=False):
            if j not in unit_grouped:
                unit_grouped[j] = units.tile([P, LEVELS, P, PACK], BF16, name="unit_grouped", align_bytes=64)
            copy = nc.vector.tensor_copy if on_vector else nc.scalar.copy
            copy(
                out=unit_grouped[j][:, span(levels)].rearrange("p l r t -> p (l r t)").bitcast(F32),
                in_=unit_turned[j, levels][:].rearrange("p l u r -> p l r u"),
            )

        def quantise_unit(j, levels=BOTH):
            if j not in unit_codes:
                unit_codes[j] = units.tile([P, LEVELS, P], U32, name="unit_codes", align_bytes=64)
                unit_scales[j] = units.tile([P, LEVELS, P], U8, name="unit_scales", align_bytes=64)
            nc.vector.quantize_mx(
                out=unit_codes[j][:, span(levels)].rearrange("p l r -> p (l r)").bitcast(FP8X4),
                scales=unit_scales[j][:, span(levels)].rearrange("p l r -> p (l r)"),
                in_=unit_grouped[j][:, span(levels)].rearrange("p l r t -> p (l r t)"),
            )

        def link_pass(j):
            nc.tensor.matmul_mx(
                out=link[:],
                lhsT=unit_codes[j][:, 0, :].bitcast(FP8X4),
                lhsT_scale=unit_scales[j][:, 0, :],
                rhs=unit_codes[j][:, 1, :].bitcast(FP8X4),
                rhs_scale=unit_scales[j][:, 1, :],
                start=(j == 0),
                stop=(j == PAIRS - 1),
            )

        def pair_at(step, lag):
            j, odd = divmod(step - lag, PAIR)
            return j if odd == 0 and 0 <= j < PAIRS else None

        load_low(0, 0, 2)
        load_high(0, 0, 1)
        load_low(0, 1, 2)
        load_high(0, 1, 1)
        load_weights()
        for b in (1, 2):
            load_low(b)
            load_high(b)
        open_low(0)
        regroup_low(0, 2)
        lift(0)
        regroup_high(0, 0, 1)
        regroup_high(0, 1, 1)
        settle(0)
        turn_weights()
        lift(1)
        quantise_low(0)
        quantise_high(0)
        quantise_weights()
        open_low(1)
        target, source = low_views(1, 0, 1)
        lower, upper = slice(SIDE // 2, SIDE), slice(0, SIDE // 2)
        nc.scalar.copy(out=target[:, lower, 1], in_=source[:, lower, 1])
        nc.vector.tensor_copy(out=target[:, :, 0], in_=source[:, :, 0])
        nc.vector.tensor_copy(out=target[:, upper, 1], in_=source[:, upper, 1])
        quantise_low(1)
        open_cam(0)
        multiply_high(0)
        multiply_low(0)
        regroup_high(1)
        settle(1)
        lift(2)

        last = BATCH - 1
        shared = set()
        for step in range(1, last):
            normed = pair_at(step, 2)
            turned = pair_at(step, 4)
            linked = pair_at(step, 5)
            sum_squares(step - 1)
            if step + 2 < BATCH:
                load_high(step + 2)
                load_low(step + 2)
            settle(step + 1)
            if normed is not None:
                clamp_squares(normed)
            regroup_high(step + 1)
            if normed is not None:
                invert_norms(normed)
            quantise_high(step)
            if step > 2:
                quantise_low(step)
            open_cam(step)
            multiply_high(step)
            multiply_low(step)
            if linked is not None and linked < PAIRS - LATE:
                quantise_unit(linked)
                link_pass(linked)
            if step + 1 not in shared:
                open_low(step + 1)
            regroup_low(step + 1, columns=SIDE - SHARE if step + 1 in shared else SIDE)
            if step == 1:
                quantise_low(step + 1)
            if step + 2 < BATCH:
                lift(step + 2)
            if turned is not None:
                regroup_unit(turned)
            if normed is not None:
                normalise(normed)
                turn(normed)
            elif 1 < step < last - 1:
                open_low(step + 2)
                share_low(step + 2)
                shared.add(step + 2)

        even, odd = (0,), (1,)
        low, high = (0,), (1,)
        j = PAIRS - 1
        sum_squares(last - 1)
        quantise_high(last)
        open_cam(last)
        multiply_high(last)
        clamp_squares(j, even)
        sum_squares(last, high)
        invert_norms(j, even)
        clamp_squares(j, odd, high)
        for w in range(N_WIN):
            quantise_low(last, w, 1)
            multiply_low(last, w, 1)
        invert_norms(j, odd, high)
        for late in range(PAIRS - LATE, j - 1):
            quantise_unit(late)
            link_pass(late)
        normalise(j, even, on_vector=True)
        normalise(j, odd, high, on_vector=True)
        turn(j, high)
        sum_squares(last, low)
        clamp_squares(j, odd, low)
        regroup_unit(j - 1, on_vector=True)
        invert_norms(j, odd, low)
        regroup_unit(j, high, on_vector=True)
        normalise(j, odd, low)
        turn(j, low)
        quantise_unit(j - 1)
        link_pass(j - 1)
        quantise_unit(j, high)
        regroup_unit(j, low)
        quantise_unit(j, low)
        link_pass(j)

        result = consts.tile([P, P], F32, name="result")
        nc.scalar.activation(out=result[:], in_=link[:], func=ACT.Copy, scale=TO_MEAN[0] / BATCH)
        nc.sync.dma_start(out=out, in_=result[:])
